import numpy as np
import ml_dtypes


def mxq(x, axis, fmt="e4m3"):
    dtype, down = {"e4m3": (ml_dtypes.float8_e4m3fn, 7), "e5m2": (ml_dtypes.float8_e5m2, 14)}[fmt]
    v = np.moveaxis(np.asarray(x, np.float32).astype(ml_dtypes.bfloat16).astype(np.float64), axis, -1)
    blocks = v.reshape(v.shape[:-1] + (-1, 32))
    amax = np.abs(blocks).max(-1, keepdims=True)
    byte = np.maximum(np.where(amax > 0, np.frexp(amax)[1] - 1 + 127, 0) - down, 1)
    scale = np.exp2(byte - 127.0)
    codes = (blocks / scale).astype(np.float32).astype(dtype).astype(np.float64)
    return np.moveaxis((codes * scale).reshape(v.shape), -1, axis)


WIDE = False


def mx_kscale(k):
    if not WIDE:
        return np.ones(k)
    levels = np.array([10, -10, 5, -5, 0])
    a = np.random.permutation(np.resize(levels, k // 512 * 4)).reshape(k // 512, 4)
    idx = np.arange(k)
    return np.exp2(a[idx // 512, idx % 128 // 32])


BF16 = ml_dtypes.bfloat16


def bf(x):
    return np.asarray(x, np.float32).astype(BF16)


def f64(x):
    return np.asarray(x).astype(np.float64)


E2M1 = np.array([0.0, 0.5, 1.0, 1.5, 2.0, 3.0, 4.0, 6.0, -0.0, -0.5, -1.0, -1.5, -2.0, -3.0, -4.0, -6.0])


def pack_weight(w, fmt):
    k, n = w.shape
    w = f64(bf(w)).reshape(k // 32, 32, n)
    amax = np.abs(w).max(1)
    if fmt == "e4m3":
        byte = np.frexp(amax)[1] - 1 + 127 - 7
    else:
        mant, ex = np.frexp(amax / 6.0)
        byte = np.where(mant > 0.5, ex, ex - 1) + 127
    byte = np.clip(np.where(amax > 0, byte, 1), 1, 254)
    scaled = (w * np.exp2(127.0 - byte)[:, None, :]).reshape(k, n).astype(np.float32)
    by_word = np.ascontiguousarray(scaled.reshape(k // 512, 128, 4, n).transpose(0, 1, 3, 2))
    if fmt == "e4m3":
        words = by_word.astype(ml_dtypes.float8_e4m3fn).view(np.uint8)
    else:
        c = by_word.astype(ml_dtypes.float4_e2m1fn).view(np.uint8) & 0xF
        words = c[..., 0::2] | (c[..., 1::2] << 4)
    return np.ascontiguousarray(words), np.ascontiguousarray(byte.astype(np.uint8).reshape(k // 512, 16, n))


def unpack_weight(words, scales, fmt):
    g, p, n, _ = words.shape
    if fmt == "e4m3":
        vals = np.ascontiguousarray(words).view(ml_dtypes.float8_e4m3fn).astype(np.float64)
    else:
        nib = np.empty((g, p, n, 4), np.uint8)
        nib[..., 0::2] = words & 0xF
        nib[..., 1::2] = words >> 4
        vals = E2M1[nib]
    vals = vals * np.repeat(np.exp2(scales.astype(np.float64) - 127.0), 8, axis=1)[..., None]
    return vals.transpose(0, 1, 3, 2).reshape(g * 512, n)

def pack4(w):
    words, scales = pack_weight(w, "e2m1")
    return words.reshape(words.shape[0], 128, -1), scales


def unpack4(words, scales):
    return unpack_weight(words.reshape(words.shape[0], 128, -1, 2), scales, "e2m1")


B, C, H, W = 128, 512, 6, 6
C3, P = 3 * C, H * W
EPS = 1e-5


def setup_inputs():
    s = mx_kscale(C3)
    n = np.random.standard_normal
    fv = bf(n((B, C3, H, W)) * s[None, :, None, None])
    ft = bf(n((B, C)))
    W1_words, W1_scales = pack4((n((C, C3)) / np.sqrt(C3) / s[None, :]).T)
    return {
        "fv": fv,
        "ft": ft,
        "W1_words": W1_words,
        "W1_scales": W1_scales,
        "b1": bf(n(C) * 0.3),
        "g1": bf(1.0 + 0.1 * n(C)),
        "be1": bf(n(C) * 0.3),
        "m1": bf(n(C) * 0.3),
        "v1": bf(np.random.uniform(0.5, 1.5, C)),
        "Wfc1": bf(n((C, C)) * 0.7 / np.sqrt(C)),
        "bfc1": bf(n(C) * 0.3),
    }


def reference(fv, ft, W1_words, W1_scales, b1, g1, be1, m1, v1, Wfc1, bfc1):
    x = (unpack4(W1_words, W1_scales).T @ mxq(f64(fv).reshape(B, C3, P), 1, "e4m3")) + f64(b1)[None, :, None]
    s = f64(g1) / np.sqrt(f64(v1) + EPS)
    fv1 = np.maximum(x * s[None, :, None] + (f64(be1) - f64(m1) * s)[None, :, None], 0.0)
    ft1 = f64(ft) @ f64(Wfc1).T + f64(bfc1)
    out = fv1 + fv1 * ft1[:, :, None]
    return out.reshape(B, C, H, W)

@@ -1,0 +1,217 @@
+from contextlib import ExitStack
+
+import concourse.mybir as mybir
+from concourse.masks import make_identity
+
+BF16 = mybir.dt.bfloat16
+F32 = mybir.dt.float32
+I32 = mybir.dt.int32
+U8 = mybir.dt.uint8
+U32 = mybir.dt.uint32
+FP8X4 = mybir.dt.float8_e4m3fn_x4
+FP4X4 = mybir.dt.float4_e2m1fn_x4
+ACT = mybir.ActivationFunctionType
+ALU = mybir.AluOpType
+
+P = 128
+PACK = 4
+B, C_IN, C_OUT, PIX = 128, 1536, 512, 36
+PASSES = C_IN // (P * PACK)
+O_TILES = C_OUT // P
+K_TILES = C_OUT // P
+EPS = 1e-5
+
+NB = 32
+CHUNKS = B // NB
+QUAD = 4
+QUADS = PIX // QUAD
+UNIT = NB * QUAD
+CHUNK_COLS = QUADS * UNIT
+UNIT_GROUPS = ((0, 4), (4, 4), (8, 1))
+VECTOR_UNITS = 6
+LOADS_AHEAD = 3
+
+FLOPS = 2 * B * PIX * C_IN * C_OUT + 2 * B * C_OUT * C_OUT
+
+
+def tile_joint_module_pa_t_kernel(
+    tc, fv, ft, W1_words, W1_scales, b1, g1, be1, m1, v1, Wfc1, bfc1, out
+):
+    nc = tc.nc
+    with ExitStack() as ctx:
+        const = ctx.enter_context(tc.tile_pool(name="const", bufs=1))
+        raw_pool = ctx.enter_context(tc.tile_pool(name="raw", bufs=4))
+        grouped_pool = ctx.enter_context(tc.tile_pool(name="grouped", bufs=3))
+        mx_pool = ctx.enter_context(tc.tile_pool(name="mx", bufs=2))
+        out_pool = ctx.enter_context(tc.tile_pool(name="outp", bufs=2))
+        acc_pool = ctx.enter_context(tc.psum_pool(name="acc", bufs=4))
+        tp_pool = ctx.enter_context(tc.psum_pool(name="tp", bufs=4))
+
+        def load_chunk_pass(chunk, g):
+            raw = raw_pool.tile([P, NB, PACK * PIX], BF16, name="raw")
+            nc.sync.dma_start(
+                out=raw[:],
+                in_=fv[
+                    chunk * NB : (chunk + 1) * NB, g * P * PACK : (g + 1) * P * PACK, :, :
+                ].rearrange("b (p t) h w -> p b (t h w)", t=PACK),
+            )
+            return raw
+
+        steps = [(chunk, g) for chunk in range(CHUNKS) for g in range(PASSES)]
+        raw_tiles = [load_chunk_pass(chunk, g) for chunk, g in steps[0:LOADS_AHEAD]]
+
+        w_words = const.tile([P, PASSES, 2 * C_OUT], U8, name="w_words", align_bytes=64)
+        nc.sync.dma_start(
+            out=w_words[:].bitcast(I32), in_=W1_words.bitcast(I32).rearrange("g p n -> p g n")
+        )
+        w_scales = const.tile([P, PASSES, C_OUT], U8, name="w_scales", align_bytes=64)
+        nc.vector.memset(w_scales[:].bitcast(I32), 0)
+        for quadrant in range(4):
+            nc.sync.dma_start(
+                out=w_scales[32 * quadrant : 32 * quadrant + 4].bitcast(I32),
+                in_=W1_scales[:, 4 * quadrant : 4 * quadrant + 4, :]
+                .bitcast(I32)
+                .rearrange("g r n -> r g n"),
+            )
+
+        ident_bf = const.tile([P, P], BF16, name="ident_bf")
+        make_identity(nc, ident_bf[:])
+        ident_f32 = const.tile([P, P], F32, name="ident_f32")
+        make_identity(nc, ident_f32[:])
+
+        vectors = (b1, g1, be1, m1, v1)
+        rows = const.tile([P, P], BF16, name="rows")
+        nc.vector.memset(rows[:], 0.0)
+        for v, vector in enumerate(vectors):
+            nc.scalar.dma_start(
+                out=rows[O_TILES * v : O_TILES * (v + 1), :],
+                in_=vector.rearrange("(r c) -> r c", c=P),
+            )
+        rows_t = tp_pool.tile([P, P], BF16, name="rows_t", tag="tp")
+        nc.tensor.transpose(rows_t[:], rows[:], ident_bf[:])
+        per_channel = const.tile([P, len(vectors), O_TILES], F32, name="per_channel")
+        nc.vector.tensor_copy(
+            out=per_channel[:].rearrange("p v o -> p (v o)"),
+            in_=rows_t[:, 0 : len(vectors) * O_TILES],
+        )
+        b1_c, g1_c, be1_c, m1_c, v1_c = [per_channel[:, v, :] for v in range(len(vectors))]
+
+        bn_scale = const.tile([P, O_TILES], F32, name="bn_scale")
+        bn_bias = const.tile([P, O_TILES], F32, name="bn_bias")
+        nc.vector.tensor_scalar_add(out=bn_scale[:], in0=v1_c, scalar1=EPS)
+        nc.scalar.sqrt(out=bn_scale[:], in_=bn_scale[:])
+        nc.vector.reciprocal(out=bn_scale[:], in_=bn_scale[:])
+        nc.vector.tensor_mul(out=bn_scale[:], in0=bn_scale[:], in1=g1_c)
+        nc.vector.tensor_sub(out=bn_bias[:], in0=b1_c, in1=m1_c)
+        nc.vector.tensor_mul(out=bn_bias[:], in0=bn_bias[:], in1=bn_scale[:])
+        nc.vector.tensor_add(out=bn_bias[:], in0=bn_bias[:], in1=be1_c)
+
+        ft_sb = const.tile([P, C_OUT], BF16, name="ft_sb")
+        nc.scalar.dma_start(out=ft_sb[:], in_=ft)
+        wfc_sb = const.tile([P, O_TILES, C_OUT], BF16, name="wfc_sb")
+        nc.scalar.dma_start(out=wfc_sb[:], in_=Wfc1.rearrange("(t o) k -> o t k", o=P))
+        bias_row = const.tile([P, C_OUT], BF16, name="bias_row")
+        nc.vector.memset(bias_row[:], 0.0)
+        nc.scalar.dma_start(out=bias_row[0:1, :], in_=bfc1.unsqueeze(0))
+        ones = const.tile([P, P], BF16, name="ones")
+        nc.vector.memset(ones[:], 1.0)
+
+        ft_t_ps = tp_pool.tile([P, K_TILES, P], BF16, name="ft_t_ps", tag="tp")
+        for kt in range(K_TILES):
+            nc.tensor.transpose(ft_t_ps[:, kt, :], ft_sb[:, kt * P : (kt + 1) * P], ident_bf[:])
+        ft_t = const.tile([P, K_TILES, P], BF16, name="ft_t")
+        nc.vector.tensor_copy(out=ft_t[:], in_=ft_t_ps[:])
+        wfc_t = const.tile([P, K_TILES, C_OUT], BF16, name="wfc_t")
+        for kt in range(K_TILES):
+            wfc_t_ps = tp_pool.tile([P, O_TILES, P], BF16, name="wfc_t_ps", tag="tp")
+            for ot in range(O_TILES):
+                nc.tensor.transpose(
+                    wfc_t_ps[:, ot, :], wfc_sb[:, ot, kt * P : (kt + 1) * P], ident_bf[:]
+                )
+            nc.vector.tensor_copy(
+                out=wfc_t[:, kt, :], in_=wfc_t_ps[:].rearrange("p t o -> p (t o)")
+            )
+        gate_ps = tp_pool.tile([P, C_OUT], F32, name="gate_ps", tag="tp")
+        nc.tensor.matmul(gate_ps[:], lhsT=ones[:], rhs=bias_row[:], start=True, stop=False)
+        for kt in range(K_TILES):
+            nc.tensor.matmul(
+                gate_ps[:],
+                lhsT=ft_t[:, kt, :],
+                rhs=wfc_t[:, kt, :],
+                start=False,
+                stop=(kt == K_TILES - 1),
+            )
+        gate = const.tile([P, C_OUT], F32, name="gate")
+        nc.vector.tensor_scalar_add(out=gate[:], in0=gate_ps[:], scalar1=1.0)
+
+        fv1 = const.tile([P, O_TILES, PIX, B], F32, name="fv1")
+
+        for chunk in range(CHUNKS):
+            codes = mx_pool.tile([P, PASSES, CHUNK_COLS], U32, name="codes", align_bytes=64)
+            scales = mx_pool.tile([P, PASSES, CHUNK_COLS], U8, name="scales", align_bytes=64)
+            for g in range(PASSES):
+                step = chunk * PASSES + g
+                raw = raw_tiles[step]
+                if step + LOADS_AHEAD < len(steps):
+                    raw_tiles.append(load_chunk_pass(*steps[step + LOADS_AHEAD]))
+                grouped = grouped_pool.tile(
+                    [P, QUADS, NB, QUAD, PACK], BF16, name="grouped", align_bytes=64
+                )
+                src = raw[:].rearrange("p b (t q l) -> p q b t l", t=PACK, l=QUAD)
+                dst = grouped[:].rearrange("p q b l t -> p q b t l")
+                nc.vector.tensor_copy(out=dst[:, 0:VECTOR_UNITS], in_=src[:, 0:VECTOR_UNITS])
+                for q in range(VECTOR_UNITS, QUADS):
+                    nc.scalar.copy(out=dst[:, q], in_=src[:, q])
+                for q0, nq in UNIT_GROUPS:
+                    cols = slice(q0 * UNIT, (q0 + nq) * UNIT)
+                    nc.vector.quantize_mx(
+                        out=codes[:, g, cols].bitcast(FP8X4),
+                        scales=scales[:, g, cols],
+                        in_=grouped[:, q0 : q0 + nq].rearrange("p q b l t -> p (q b l t)"),
+                    )
+
+            for ot in range(O_TILES):
+                for q0, nq in UNIT_GROUPS:
+                    cols = slice(q0 * UNIT, (q0 + nq) * UNIT)
+                    acc = acc_pool.tile([P, 4 * UNIT], F32, name="acc")
+                    for g in range(PASSES):
+                        nc.tensor.matmul_mx(
+                            out=acc[:, 0 : nq * UNIT],
+                            lhsT=w_words[:, g, 2 * P * ot : 2 * P * (ot + 1)].bitcast(FP4X4),
+                            lhsT_scale=w_scales[:, g, P * ot : P * (ot + 1)],
+                            rhs=codes[:, g, cols].bitcast(FP8X4),
+                            rhs_scale=scales[:, g, cols],
+                            start=(g == 0),
+                            stop=(g == PASSES - 1),
+                        )
+                    nc.scalar.activation(
+                        out=fv1[
+                            :, ot, q0 * QUAD : (q0 + nq) * QUAD, chunk * NB : (chunk + 1) * NB
+                        ].rearrange("p (q l) b -> p q l b", l=QUAD),
+                        in_=acc[:, 0 : nq * UNIT].rearrange(
+                            "p (q b l) -> p q l b", b=NB, l=QUAD
+                        ),
+                        func=ACT.Relu,
+                        scale=bn_scale[:, ot : ot + 1],
+                        bias=bn_bias[:, ot : ot + 1],
+                    )
+
+        for ot in range(O_TILES):
+            gate_ot = gate[:, ot * P : (ot + 1) * P].unsqueeze(2).to_broadcast([P, P, QUAD])
+            result = out_pool.tile([P, P, PIX], F32, name="result")
+            for q in range(QUADS):
+                flipped = tp_pool.tile([P, QUAD, P], F32, name="flipped", tag="tp")
+                for lane in range(QUAD):
+                    nc.tensor.transpose(
+                        flipped[:, lane, :], fv1[:, ot, q * QUAD + lane, :], ident_f32[:]
+                    )
+                nc.vector.tensor_tensor(
+                    out=result[:, :, q * QUAD : (q + 1) * QUAD],
+                    in0=flipped[:].rearrange("p l o -> p o l"),
+                    in1=gate_ot,
+                    op=ALU.mult,
+                )
+            nc.sync.dma_start(
+                out=out[:, ot * P : (ot + 1) * P, :, :].rearrange("b o h w -> b (o h w)"),
+                in_=result[:].rearrange("p o x -> p (o x)"),
+            )

@@ -21,7 +21,9 @@ O_TILES = C_OUT // P
 K_TILES = C_OUT // P
 EPS = 1e-5
 
-NB = 32
+OCTETS = 4
+MEMBERS = 8
+NB = OCTETS * MEMBERS
 CHUNKS = B // NB
 QUAD = 4
 QUADS = PIX // QUAD
@@ -29,7 +31,8 @@ UNIT = NB * QUAD
 CHUNK_COLS = QUADS * UNIT
 UNIT_GROUPS = ((0, 4), (4, 4), (8, 1))
 VECTOR_UNITS = 6
-LOADS_AHEAD = 3
+RAW_BUFS = 6
+LOADS_AHEAD = RAW_BUFS - 1
 
 FLOPS = 2 * B * PIX * C_IN * C_OUT + 2 * B * C_OUT * C_OUT
 
@@ -40,25 +43,28 @@ def tile_joint_module_pa_t_kernel(
     nc = tc.nc
     with ExitStack() as ctx:
         const = ctx.enter_context(tc.tile_pool(name="const", bufs=1))
-        raw_pool = ctx.enter_context(tc.tile_pool(name="raw", bufs=4))
+        raw_pool = ctx.enter_context(tc.tile_pool(name="raw", bufs=RAW_BUFS))
         grouped_pool = ctx.enter_context(tc.tile_pool(name="grouped", bufs=3))
         mx_pool = ctx.enter_context(tc.tile_pool(name="mx", bufs=2))
+        fv1_pool = ctx.enter_context(tc.tile_pool(name="fv1", bufs=2))
         out_pool = ctx.enter_context(tc.tile_pool(name="outp", bufs=2))
         acc_pool = ctx.enter_context(tc.psum_pool(name="acc", bufs=4))
         tp_pool = ctx.enter_context(tc.psum_pool(name="tp", bufs=4))
 
         def load_chunk_pass(chunk, g):
             raw = raw_pool.tile([P, NB, PACK * PIX], BF16, name="raw")
-            nc.sync.dma_start(
-                out=raw[:],
-                in_=fv[
-                    chunk * NB : (chunk + 1) * NB, g * P * PACK : (g + 1) * P * PACK, :, :
-                ].rearrange("b (p t) h w -> p b (t h w)", t=PACK),
-            )
+            for octet in range(OCTETS):
+                first = chunk * NB + octet * MEMBERS
+                nc.sync.dma_start(
+                    out=raw[:, octet:NB:OCTETS, :],
+                    in_=fv[
+                        first : first + MEMBERS, g * P * PACK : (g + 1) * P * PACK, :, :
+                    ].rearrange("b (p t) h w -> p b (t h w)", t=PACK),
+                )
             return raw
 
         steps = [(chunk, g) for chunk in range(CHUNKS) for g in range(PASSES)]
-        raw_tiles = [load_chunk_pass(chunk, g) for chunk, g in steps[0:LOADS_AHEAD]]
+        raw_tiles = [load_chunk_pass(chunk, g) for chunk, g in steps[0:1]]
 
         w_words = const.tile([P, PASSES, 2 * C_OUT], U8, name="w_words", align_bytes=64)
         nc.sync.dma_start(
@@ -73,13 +79,14 @@ def tile_joint_module_pa_t_kernel(
                 .bitcast(I32)
                 .rearrange("g r n -> r g n"),
             )
+        raw_tiles.extend([load_chunk_pass(chunk, g) for chunk, g in steps[1:LOADS_AHEAD]])
 
         ident_bf = const.tile([P, P], BF16, name="ident_bf")
         make_identity(nc, ident_bf[:])
         ident_f32 = const.tile([P, P], F32, name="ident_f32")
         make_identity(nc, ident_f32[:])
 
-        vectors = (b1, g1, be1, m1, v1)
+        vectors = (b1, g1, be1, m1, v1, bfc1)
         rows = const.tile([P, P], BF16, name="rows")
         nc.vector.memset(rows[:], 0.0)
         for v, vector in enumerate(vectors):
@@ -94,7 +101,9 @@ def tile_joint_module_pa_t_kernel(
             out=per_channel[:].rearrange("p v o -> p (v o)"),
             in_=rows_t[:, 0 : len(vectors) * O_TILES],
         )
-        b1_c, g1_c, be1_c, m1_c, v1_c = [per_channel[:, v, :] for v in range(len(vectors))]
+        b1_c, g1_c, be1_c, m1_c, v1_c, bfc1_c = [
+            per_channel[:, v, :] for v in range(len(vectors))
+        ]
 
         bn_scale = const.tile([P, O_TILES], F32, name="bn_scale")
         bn_bias = const.tile([P, O_TILES], F32, name="bn_bias")
@@ -105,16 +114,13 @@ def tile_joint_module_pa_t_kernel(
         nc.vector.tensor_sub(out=bn_bias[:], in0=b1_c, in1=m1_c)
         nc.vector.tensor_mul(out=bn_bias[:], in0=bn_bias[:], in1=bn_scale[:])
         nc.vector.tensor_add(out=bn_bias[:], in0=bn_bias[:], in1=be1_c)
+        gate_bias = const.tile([P, O_TILES], F32, name="gate_bias")
+        nc.vector.tensor_scalar_add(out=gate_bias[:], in0=bfc1_c, scalar1=1.0)
 
         ft_sb = const.tile([P, C_OUT], BF16, name="ft_sb")
         nc.scalar.dma_start(out=ft_sb[:], in_=ft)
         wfc_sb = const.tile([P, O_TILES, C_OUT], BF16, name="wfc_sb")
         nc.scalar.dma_start(out=wfc_sb[:], in_=Wfc1.rearrange("(t o) k -> o t k", o=P))
-        bias_row = const.tile([P, C_OUT], BF16, name="bias_row")
-        nc.vector.memset(bias_row[:], 0.0)
-        nc.scalar.dma_start(out=bias_row[0:1, :], in_=bfc1.unsqueeze(0))
-        ones = const.tile([P, P], BF16, name="ones")
-        nc.vector.memset(ones[:], 1.0)
 
         ft_t_ps = tp_pool.tile([P, K_TILES, P], BF16, name="ft_t_ps", tag="tp")
         for kt in range(K_TILES):
@@ -131,20 +137,33 @@ def tile_joint_module_pa_t_kernel(
             nc.vector.tensor_copy(
                 out=wfc_t[:, kt, :], in_=wfc_t_ps[:].rearrange("p t o -> p (t o)")
             )
-        gate_ps = tp_pool.tile([P, C_OUT], F32, name="gate_ps", tag="tp")
-        nc.tensor.matmul(gate_ps[:], lhsT=ones[:], rhs=bias_row[:], start=True, stop=False)
-        for kt in range(K_TILES):
-            nc.tensor.matmul(
-                gate_ps[:],
-                lhsT=ft_t[:, kt, :],
-                rhs=wfc_t[:, kt, :],
-                start=False,
-                stop=(kt == K_TILES - 1),
+        gate_t = const.tile([P, CHUNKS, MEMBERS, O_TILES, OCTETS], F32, name="gate_t")
+        for ot in range(O_TILES):
+            gate_t_ps = tp_pool.tile([P, B], F32, name="gate_t_ps", tag="tp")
+            for kt in range(K_TILES):
+                nc.tensor.matmul(
+                    gate_t_ps[:],
+                    lhsT=wfc_t[:, kt, ot * P : (ot + 1) * P],
+                    rhs=ft_t[:, kt, :],
+                    start=(kt == 0),
+                    stop=(kt == K_TILES - 1),
+                )
+            nc.vector.tensor_scalar_add(
+                out=gate_t[:, :, :, ot, :],
+                in0=gate_t_ps[:].rearrange(
+                    "p (c r m) -> p c m r", r=OCTETS, m=MEMBERS
+                ),
+                scalar1=gate_bias[:, ot : ot + 1],
             )
-        gate = const.tile([P, C_OUT], F32, name="gate")
-        nc.vector.tensor_scalar_add(out=gate[:], in0=gate_ps[:], scalar1=1.0)
-
-        fv1 = const.tile([P, O_TILES, PIX, B], F32, name="fv1")
+        gate_ps = tp_pool.tile([P, CHUNKS, P], F32, name="gate_ps", tag="tp")
+        for chunk in range(CHUNKS):
+            nc.tensor.transpose(
+                gate_ps[:, chunk, :],
+                gate_t[:, chunk].rearrange("p m t r -> p (m t r)"),
+                ident_f32[:],
+            )
+        gate = const.tile([P, CHUNKS, P], F32, name="gate")
+        nc.vector.tensor_copy(out=gate[:], in_=gate_ps[:])
 
         for chunk in range(CHUNKS):
             codes = mx_pool.tile([P, PASSES, CHUNK_COLS], U32, name="codes", align_bytes=64)
@@ -157,8 +176,8 @@ def tile_joint_module_pa_t_kernel(
                 grouped = grouped_pool.tile(
                     [P, QUADS, NB, QUAD, PACK], BF16, name="grouped", align_bytes=64
                 )
-                src = raw[:].rearrange("p b (t q l) -> p q b t l", t=PACK, l=QUAD)
-                dst = grouped[:].rearrange("p q b l t -> p q b t l")
+                src = raw[:].rearrange("p s (t q l) -> p q s t l", t=PACK, l=QUAD)
+                dst = grouped[:].rearrange("p q s l t -> p q s t l")
                 nc.vector.tensor_copy(out=dst[:, 0:VECTOR_UNITS], in_=src[:, 0:VECTOR_UNITS])
                 for q in range(VECTOR_UNITS, QUADS):
                     nc.scalar.copy(out=dst[:, q], in_=src[:, q])
@@ -167,9 +186,10 @@ def tile_joint_module_pa_t_kernel(
                     nc.vector.quantize_mx(
                         out=codes[:, g, cols].bitcast(FP8X4),
                         scales=scales[:, g, cols],
-                        in_=grouped[:, q0 : q0 + nq].rearrange("p q b l t -> p (q b l t)"),
+                        in_=grouped[:, q0 : q0 + nq].rearrange("p q s l t -> p (q s l t)"),
                     )
 
+            fv1 = fv1_pool.tile([P, PIX, MEMBERS, O_TILES, OCTETS], F32, name="fv1")
             for ot in range(O_TILES):
                 for q0, nq in UNIT_GROUPS:
                     cols = slice(q0 * UNIT, (q0 + nq) * UNIT)
@@ -185,33 +205,38 @@ def tile_joint_module_pa_t_kernel(
                             stop=(g == PASSES - 1),
                         )
                     nc.scalar.activation(
-                        out=fv1[
-                            :, ot, q0 * QUAD : (q0 + nq) * QUAD, chunk * NB : (chunk + 1) * NB
-                        ].rearrange("p (q l) b -> p q l b", l=QUAD),
+                        out=fv1[:, q0 * QUAD : (q0 + nq) * QUAD, :, ot, :].rearrange(
+                            "p (q l) m r -> p q l m r", l=QUAD
+                        ),
                         in_=acc[:, 0 : nq * UNIT].rearrange(
-                            "p (q b l) -> p q l b", b=NB, l=QUAD
+                            "p (q m r l) -> p q l m r", m=MEMBERS, r=OCTETS, l=QUAD
                         ),
                         func=ACT.Relu,
                         scale=bn_scale[:, ot : ot + 1],
                         bias=bn_bias[:, ot : ot + 1],
                     )
 
-        for ot in range(O_TILES):
-            gate_ot = gate[:, ot * P : (ot + 1) * P].unsqueeze(2).to_broadcast([P, P, QUAD])
+            gate_chunk = gate[:, chunk, :].unsqueeze(2).to_broadcast([P, P, QUAD])
             result = out_pool.tile([P, P, PIX], F32, name="result")
             for q in range(QUADS):
                 flipped = tp_pool.tile([P, QUAD, P], F32, name="flipped", tag="tp")
                 for lane in range(QUAD):
                     nc.tensor.transpose(
-                        flipped[:, lane, :], fv1[:, ot, q * QUAD + lane, :], ident_f32[:]
+                        flipped[:, lane, :],
+                        fv1[:, q * QUAD + lane].rearrange("p m t r -> p (m t r)"),
+                        ident_f32[:],
                     )
                 nc.vector.tensor_tensor(
                     out=result[:, :, q * QUAD : (q + 1) * QUAD],
                     in0=flipped[:].rearrange("p l o -> p o l"),
-                    in1=gate_ot,
+                    in1=gate_chunk,
                     op=ALU.mult,
                 )
-            nc.sync.dma_start(
-                out=out[:, ot * P : (ot + 1) * P, :, :].rearrange("b o h w -> b (o h w)"),
-                in_=result[:].rearrange("p o x -> p (o x)"),
-            )
+            for octet in range(OCTETS):
+                first = chunk * NB + octet * MEMBERS
+                nc.sync.dma_start(
+                    out=out[first : first + MEMBERS].rearrange(
+                        "b (t o) h w -> (b t) (o h w)", t=O_TILES
+                    ),
+                    in_=result[octet:P:OCTETS].rearrange("p o x -> p (o x)"),
+                )

@@ -31,7 +31,7 @@ UNIT = NB * QUAD
 CHUNK_COLS = QUADS * UNIT
 UNIT_GROUPS = ((0, 4), (4, 4), (8, 1))
 VECTOR_UNITS = 6
-RAW_BUFS = 6
+RAW_BUFS = 4
 LOADS_AHEAD = RAW_BUFS - 1
 
 FLOPS = 2 * B * PIX * C_IN * C_OUT + 2 * B * C_OUT * C_OUT
@@ -42,12 +42,13 @@ def tile_joint_module_pa_t_kernel(
 ):
     nc = tc.nc
     with ExitStack() as ctx:
+        ctx.enter_context(tc.manual_schedule())
         const = ctx.enter_context(tc.tile_pool(name="const", bufs=1))
         raw_pool = ctx.enter_context(tc.tile_pool(name="raw", bufs=RAW_BUFS))
         grouped_pool = ctx.enter_context(tc.tile_pool(name="grouped", bufs=3))
         mx_pool = ctx.enter_context(tc.tile_pool(name="mx", bufs=2))
         fv1_pool = ctx.enter_context(tc.tile_pool(name="fv1", bufs=2))
-        out_pool = ctx.enter_context(tc.tile_pool(name="outp", bufs=2))
+        out_pool = ctx.enter_context(tc.tile_pool(name="outp", bufs=CHUNKS))
         acc_pool = ctx.enter_context(tc.psum_pool(name="acc", bufs=4))
         tp_pool = ctx.enter_context(tc.psum_pool(name="tp", bufs=4))
 
@@ -94,6 +95,11 @@ def tile_joint_module_pa_t_kernel(
                 out=rows[O_TILES * v : O_TILES * (v + 1), :],
                 in_=vector.rearrange("(r c) -> r c", c=P),
             )
+        ft_sb = const.tile([P, C_OUT], BF16, name="ft_sb")
+        nc.scalar.dma_start(out=ft_sb[:], in_=ft)
+        wfc_sb = const.tile([P, O_TILES, C_OUT], BF16, name="wfc_sb")
+        nc.scalar.dma_start(out=wfc_sb[:], in_=Wfc1.rearrange("(t o) k -> o t k", o=P))
+
         rows_t = tp_pool.tile([P, P], BF16, name="rows_t", tag="tp")
         nc.tensor.transpose(rows_t[:], rows[:], ident_bf[:])
         per_channel = const.tile([P, len(vectors), O_TILES], F32, name="per_channel")
@@ -116,11 +122,6 @@ def tile_joint_module_pa_t_kernel(
         nc.vector.tensor_add(out=bn_bias[:], in0=bn_bias[:], in1=be1_c)
         gate_bias = const.tile([P, O_TILES], F32, name="gate_bias")
         nc.vector.tensor_scalar_add(out=gate_bias[:], in0=bfc1_c, scalar1=1.0)
-
-        ft_sb = const.tile([P, C_OUT], BF16, name="ft_sb")
-        nc.scalar.dma_start(out=ft_sb[:], in_=ft)
-        wfc_sb = const.tile([P, O_TILES, C_OUT], BF16, name="wfc_sb")
-        nc.scalar.dma_start(out=wfc_sb[:], in_=Wfc1.rearrange("(t o) k -> o t k", o=P))
 
         ft_t_ps = tp_pool.tile([P, K_TILES, P], BF16, name="ft_t_ps", tag="tp")
         for kt in range(K_TILES):
@@ -165,60 +166,78 @@ def tile_joint_module_pa_t_kernel(
         gate = const.tile([P, CHUNKS, P], F32, name="gate")
         nc.vector.tensor_copy(out=gate[:], in_=gate_ps[:])
 
-        for chunk in range(CHUNKS):
-            codes = mx_pool.tile([P, PASSES, CHUNK_COLS], U32, name="codes", align_bytes=64)
-            scales = mx_pool.tile([P, PASSES, CHUNK_COLS], U8, name="scales", align_bytes=64)
-            for g in range(PASSES):
-                step = chunk * PASSES + g
-                raw = raw_tiles[step]
-                if step + LOADS_AHEAD < len(steps):
-                    raw_tiles.append(load_chunk_pass(*steps[step + LOADS_AHEAD]))
-                grouped = grouped_pool.tile(
-                    [P, QUADS, NB, QUAD, PACK], BF16, name="grouped", align_bytes=64
+        mx_tiles = {}
+        fv1_tiles = {}
+        result_tiles = {}
+
+        def quantise_pass(chunk, g):
+            if g == 0:
+                mx_tiles[chunk] = (
+                    mx_pool.tile([P, PASSES, CHUNK_COLS], U32, name="codes", align_bytes=64),
+                    mx_pool.tile([P, PASSES, CHUNK_COLS], U8, name="scales", align_bytes=64),
                 )
-                src = raw[:].rearrange("p s (t q l) -> p q s t l", t=PACK, l=QUAD)
-                dst = grouped[:].rearrange("p q s l t -> p q s t l")
-                nc.vector.tensor_copy(out=dst[:, 0:VECTOR_UNITS], in_=src[:, 0:VECTOR_UNITS])
-                for q in range(VECTOR_UNITS, QUADS):
-                    nc.scalar.copy(out=dst[:, q], in_=src[:, q])
-                for q0, nq in UNIT_GROUPS:
-                    cols = slice(q0 * UNIT, (q0 + nq) * UNIT)
-                    nc.vector.quantize_mx(
-                        out=codes[:, g, cols].bitcast(FP8X4),
-                        scales=scales[:, g, cols],
-                        in_=grouped[:, q0 : q0 + nq].rearrange("p q s l t -> p (q s l t)"),
-                    )
+            codes, scales = mx_tiles[chunk]
+            step = chunk * PASSES + g
+            raw = raw_tiles[step]
+            if step + LOADS_AHEAD < len(steps):
+                raw_tiles.append(load_chunk_pass(*steps[step + LOADS_AHEAD]))
+            grouped = grouped_pool.tile(
+                [P, QUADS, NB, QUAD, PACK], BF16, name="grouped", align_bytes=64
+            )
+            src = raw[:].rearrange("p s (t q l) -> p q s t l", t=PACK, l=QUAD)
+            dst = grouped[:].rearrange("p q s l t -> p q s t l")
+            nc.vector.tensor_copy(out=dst[:, 0:VECTOR_UNITS], in_=src[:, 0:VECTOR_UNITS])
+            for q in range(VECTOR_UNITS, QUADS):
+                nc.scalar.copy(out=dst[:, q], in_=src[:, q])
+            for q0, nq in UNIT_GROUPS:
+                cols = slice(q0 * UNIT, (q0 + nq) * UNIT)
+                nc.vector.quantize_mx(
+                    out=codes[:, g, cols].bitcast(FP8X4),
+                    scales=scales[:, g, cols],
+                    in_=grouped[:, q0 : q0 + nq].rearrange("p q s l t -> p (q s l t)"),
+                )
 
-            fv1 = fv1_pool.tile([P, PIX, MEMBERS, O_TILES, OCTETS], F32, name="fv1")
+        def convolve(chunk, group):
+            if group == 0:
+                fv1_tiles[chunk] = fv1_pool.tile(
+                    [P, PIX, MEMBERS, O_TILES, OCTETS], F32, name="fv1"
+                )
+            fv1 = fv1_tiles[chunk]
+            codes, scales = mx_tiles[chunk]
+            q0, nq = UNIT_GROUPS[group]
+            cols = slice(q0 * UNIT, (q0 + nq) * UNIT)
             for ot in range(O_TILES):
-                for q0, nq in UNIT_GROUPS:
-                    cols = slice(q0 * UNIT, (q0 + nq) * UNIT)
-                    acc = acc_pool.tile([P, 4 * UNIT], F32, name="acc")
-                    for g in range(PASSES):
-                        nc.tensor.matmul_mx(
-                            out=acc[:, 0 : nq * UNIT],
-                            lhsT=w_words[:, g, 2 * P * ot : 2 * P * (ot + 1)].bitcast(FP4X4),
-                            lhsT_scale=w_scales[:, g, P * ot : P * (ot + 1)],
-                            rhs=codes[:, g, cols].bitcast(FP8X4),
-                            rhs_scale=scales[:, g, cols],
-                            start=(g == 0),
-                            stop=(g == PASSES - 1),
-                        )
-                    nc.scalar.activation(
-                        out=fv1[:, q0 * QUAD : (q0 + nq) * QUAD, :, ot, :].rearrange(
-                            "p (q l) m r -> p q l m r", l=QUAD
-                        ),
-                        in_=acc[:, 0 : nq * UNIT].rearrange(
-                            "p (q m r l) -> p q l m r", m=MEMBERS, r=OCTETS, l=QUAD
-                        ),
-                        func=ACT.Relu,
-                        scale=bn_scale[:, ot : ot + 1],
-                        bias=bn_bias[:, ot : ot + 1],
+                acc = acc_pool.tile([P, 4 * UNIT], F32, name="acc")
+                for g in range(PASSES):
+                    nc.tensor.matmul_mx(
+                        out=acc[:, 0 : nq * UNIT],
+                        lhsT=w_words[:, g, 2 * P * ot : 2 * P * (ot + 1)].bitcast(FP4X4),
+                        lhsT_scale=w_scales[:, g, P * ot : P * (ot + 1)],
+                        rhs=codes[:, g, cols].bitcast(FP8X4),
+                        rhs_scale=scales[:, g, cols],
+                        start=(g == 0),
+                        stop=(g == PASSES - 1),
                     )
+                nc.scalar.activation(
+                    out=fv1[:, q0 * QUAD : (q0 + nq) * QUAD, :, ot, :].rearrange(
+                        "p (q l) m r -> p q l m r", l=QUAD
+                    ),
+                    in_=acc[:, 0 : nq * UNIT].rearrange(
+                        "p (q m r l) -> p q l m r", m=MEMBERS, r=OCTETS, l=QUAD
+                    ),
+                    func=ACT.Relu,
+                    scale=bn_scale[:, ot : ot + 1],
+                    bias=bn_bias[:, ot : ot + 1],
+                )
 
+        def flip(chunk, group):
+            if group == 0:
+                result_tiles[chunk] = out_pool.tile([P, P, PIX], F32, name="result")
+            result = result_tiles[chunk]
+            fv1 = fv1_tiles[chunk]
             gate_chunk = gate[:, chunk, :].unsqueeze(2).to_broadcast([P, P, QUAD])
-            result = out_pool.tile([P, P, PIX], F32, name="result")
-            for q in range(QUADS):
+            q0, nq = UNIT_GROUPS[group]
+            for q in range(q0, q0 + nq):
                 flipped = tp_pool.tile([P, QUAD, P], F32, name="flipped", tag="tp")
                 for lane in range(QUAD):
                     nc.tensor.transpose(
@@ -232,11 +251,30 @@ def tile_joint_module_pa_t_kernel(
                     in1=gate_chunk,
                     op=ALU.mult,
                 )
+
+        def quantise_next(chunk, g):
+            if chunk + 1 < CHUNKS:
+                quantise_pass(chunk + 1, g)
+
+        for g in range(PASSES):
+            quantise_pass(0, g)
+        for chunk in range(CHUNKS):
+            convolve(chunk, 0)
+            quantise_next(chunk, 0)
+            convolve(chunk, 1)
+            quantise_next(chunk, 1)
+            flip(chunk, 0)
+            convolve(chunk, 2)
+            quantise_next(chunk, 2)
+            flip(chunk, 1)
+            flip(chunk, 2)
+
+        for chunk in range(CHUNKS):
             for octet in range(OCTETS):
                 first = chunk * NB + octet * MEMBERS
                 nc.sync.dma_start(
                     out=out[first : first + MEMBERS].rearrange(
                         "b (t o) h w -> (b t) (o h w)", t=O_TILES
                     ),
-                    in_=result[octet:P:OCTETS].rearrange("p o x -> p (o x)"),
+                    in_=result_tiles[chunk][octet:P:OCTETS].rearrange("p o x -> p (o x)"),
                 )

@@ -31,7 +31,7 @@ UNIT = NB * QUAD
 CHUNK_COLS = QUADS * UNIT
 UNIT_GROUPS = ((0, 4), (4, 4), (8, 1))
 VECTOR_UNITS = 6
-RAW_BUFS = 4
+RAW_BUFS = 6
 LOADS_AHEAD = RAW_BUFS - 1
 
 FLOPS = 2 * B * PIX * C_IN * C_OUT + 2 * B * C_OUT * C_OUT
@@ -48,7 +48,7 @@ def tile_joint_module_pa_t_kernel(
         grouped_pool = ctx.enter_context(tc.tile_pool(name="grouped", bufs=3))
         mx_pool = ctx.enter_context(tc.tile_pool(name="mx", bufs=2))
         fv1_pool = ctx.enter_context(tc.tile_pool(name="fv1", bufs=2))
-        out_pool = ctx.enter_context(tc.tile_pool(name="outp", bufs=CHUNKS))
+        out_pool = ctx.enter_context(tc.tile_pool(name="outp", bufs=3))
         acc_pool = ctx.enter_context(tc.psum_pool(name="acc", bufs=4))
         tp_pool = ctx.enter_context(tc.psum_pool(name="tp", bufs=4))
 
@@ -206,11 +206,11 @@ def tile_joint_module_pa_t_kernel(
             codes, scales = mx_tiles[chunk]
             q0, nq = UNIT_GROUPS[group]
             cols = slice(q0 * UNIT, (q0 + nq) * UNIT)
-            for ot in range(O_TILES):
-                acc = acc_pool.tile([P, 4 * UNIT], F32, name="acc")
-                for g in range(PASSES):
+            accs = [acc_pool.tile([P, 4 * UNIT], F32, name="acc") for ot in range(O_TILES)]
+            for g in range(PASSES):
+                for ot in range(O_TILES):
                     nc.tensor.matmul_mx(
-                        out=acc[:, 0 : nq * UNIT],
+                        out=accs[ot][:, 0 : nq * UNIT],
                         lhsT=w_words[:, g, 2 * P * ot : 2 * P * (ot + 1)].bitcast(FP4X4),
                         lhsT_scale=w_scales[:, g, P * ot : P * (ot + 1)],
                         rhs=codes[:, g, cols].bitcast(FP8X4),
@@ -218,11 +218,12 @@ def tile_joint_module_pa_t_kernel(
                         start=(g == 0),
                         stop=(g == PASSES - 1),
                     )
+            for ot in range(O_TILES):
                 nc.scalar.activation(
                     out=fv1[:, q0 * QUAD : (q0 + nq) * QUAD, :, ot, :].rearrange(
                         "p (q l) m r -> p q l m r", l=QUAD
                     ),
-                    in_=acc[:, 0 : nq * UNIT].rearrange(
+                    in_=accs[ot][:, 0 : nq * UNIT].rearrange(
                         "p (q m r l) -> p q l m r", m=MEMBERS, r=OCTETS, l=QUAD
                     ),
                     func=ACT.Relu,
@@ -259,15 +260,15 @@ def tile_joint_module_pa_t_kernel(
         for g in range(PASSES):
             quantise_pass(0, g)
         for chunk in range(CHUNKS):
-            convolve(chunk, 0)
             quantise_next(chunk, 0)
-            convolve(chunk, 1)
+            convolve(chunk, 0)
             quantise_next(chunk, 1)
+            convolve(chunk, 1)
             flip(chunk, 0)
             convolve(chunk, 2)
+            flip(chunk, 2)
             quantise_next(chunk, 2)
             flip(chunk, 1)
-            flip(chunk, 2)
 
         for chunk in range(CHUNKS):
             for octet in range(OCTETS):

@@ -231,14 +231,13 @@ def tile_joint_module_pa_t_kernel(
                     bias=bn_bias[:, ot : ot + 1],
                 )
 
-        def flip(chunk, group):
-            if group == 0:
+        def flip(chunk, third):
+            if third == 0:
                 result_tiles[chunk] = out_pool.tile([P, P, PIX], F32, name="result")
             result = result_tiles[chunk]
             fv1 = fv1_tiles[chunk]
             gate_chunk = gate[:, chunk, :].unsqueeze(2).to_broadcast([P, P, QUAD])
-            q0, nq = UNIT_GROUPS[group]
-            for q in range(q0, q0 + nq):
+            for q in range(third * QUADS // PASSES, (third + 1) * QUADS // PASSES):
                 flipped = tp_pool.tile([P, QUAD, P], F32, name="flipped", tag="tp")
                 for lane in range(QUAD):
                     nc.tensor.transpose(
@@ -260,15 +259,12 @@ def tile_joint_module_pa_t_kernel(
         for g in range(PASSES):
             quantise_pass(0, g)
         for chunk in range(CHUNKS):
-            quantise_next(chunk, 0)
-            convolve(chunk, 0)
-            quantise_next(chunk, 1)
-            convolve(chunk, 1)
-            flip(chunk, 0)
-            convolve(chunk, 2)
-            flip(chunk, 2)
-            quantise_next(chunk, 2)
-            flip(chunk, 1)
+            for slot in range(PASSES):
+                quantise_next(chunk, slot)
+                convolve(chunk, slot)
+                if (chunk, slot) != (0, 0):
+                    flip(*divmod(chunk * PASSES + slot - 1, PASSES))
+        flip(CHUNKS - 1, PASSES - 1)
 
         for chunk in range(CHUNKS):
             for octet in range(OCTETS):

@@ -31,8 +31,10 @@ UNIT = NB * QUAD
 CHUNK_COLS = QUADS * UNIT
 UNIT_GROUPS = ((0, 4), (4, 4), (8, 1))
 VECTOR_UNITS = 6
-RAW_BUFS = 6
-LOADS_AHEAD = RAW_BUFS - 1
+RAW_BUFS = 4
+TURNED = ((0, 0), (0, 1), (0, 2), (1, 0))
+RESULT_BYTES = P * PIX * 4
+HALF = 2
 
 FLOPS = 2 * B * PIX * C_IN * C_OUT + 2 * B * C_OUT * C_OUT
 
@@ -44,11 +46,10 @@ def tile_joint_module_pa_t_kernel(
     with ExitStack() as ctx:
         ctx.enter_context(tc.manual_schedule())
         const = ctx.enter_context(tc.tile_pool(name="const", bufs=1))
+        big_pool = ctx.enter_context(tc.tile_pool(name="big", bufs=1))
         raw_pool = ctx.enter_context(tc.tile_pool(name="raw", bufs=RAW_BUFS))
         grouped_pool = ctx.enter_context(tc.tile_pool(name="grouped", bufs=3))
         mx_pool = ctx.enter_context(tc.tile_pool(name="mx", bufs=2))
-        fv1_pool = ctx.enter_context(tc.tile_pool(name="fv1", bufs=2))
-        out_pool = ctx.enter_context(tc.tile_pool(name="outp", bufs=3))
         acc_pool = ctx.enter_context(tc.psum_pool(name="acc", bufs=4))
         tp_pool = ctx.enter_context(tc.psum_pool(name="tp", bufs=4))
 
@@ -64,131 +65,193 @@ def tile_joint_module_pa_t_kernel(
                 )
             return raw
 
-        steps = [(chunk, g) for chunk in range(CHUNKS) for g in range(PASSES)]
-        raw_tiles = [load_chunk_pass(chunk, g) for chunk, g in steps[0:1]]
+        prep_pool = tc.tile_pool(name="prep", bufs=1)
+        with prep_pool as prep:
+            vectors = (b1, g1, be1, m1, v1, bfc1)
+            rows = prep.tile([P, P], BF16, name="rows")
+            nc.vector.memset(rows[:], 0.0)
+            for v, vector in enumerate(vectors):
+                nc.sync.dma_start(
+                    out=rows[O_TILES * v : O_TILES * (v + 1), :],
+                    in_=vector.rearrange("(r c) -> r c", c=P),
+                )
+            ft_sb = prep.tile([P, C_OUT], BF16, name="ft_sb")
+            nc.sync.dma_start(out=ft_sb[:], in_=ft)
+            wfc_sb = prep.tile([P, O_TILES, C_OUT], BF16, name="wfc_sb")
+            nc.sync.dma_start(out=wfc_sb[:], in_=Wfc1.rearrange("(t o) k -> o t k", o=P))
 
-        w_words = const.tile([P, PASSES, 2 * C_OUT], U8, name="w_words", align_bytes=64)
-        nc.sync.dma_start(
-            out=w_words[:].bitcast(I32), in_=W1_words.bitcast(I32).rearrange("g p n -> p g n")
-        )
-        w_scales = const.tile([P, PASSES, C_OUT], U8, name="w_scales", align_bytes=64)
-        nc.vector.memset(w_scales[:].bitcast(I32), 0)
-        for quadrant in range(4):
+            whole = big_pool.tile([P, P * PACK * PIX], BF16, name="whole", offset=0)
+            for k, (chunk, g) in enumerate(TURNED):
+                nc.sync.dma_start(
+                    out=whole[k : P : len(TURNED), :],
+                    in_=fv[
+                        chunk * NB : (chunk + 1) * NB, g * P * PACK : (g + 1) * P * PACK, :, :
+                    ].rearrange("b c h w -> b (c h w)"),
+                )
+
+            w_words = const.tile([P, PASSES, 2 * C_OUT], U8, name="w_words", align_bytes=64)
             nc.sync.dma_start(
-                out=w_scales[32 * quadrant : 32 * quadrant + 4].bitcast(I32),
-                in_=W1_scales[:, 4 * quadrant : 4 * quadrant + 4, :]
-                .bitcast(I32)
-                .rearrange("g r n -> r g n"),
+                out=w_words[:].bitcast(I32), in_=W1_words.bitcast(I32).rearrange("g p n -> p g n")
             )
-        raw_tiles.extend([load_chunk_pass(chunk, g) for chunk, g in steps[1:LOADS_AHEAD]])
-
-        ident_bf = const.tile([P, P], BF16, name="ident_bf")
-        make_identity(nc, ident_bf[:])
-        ident_f32 = const.tile([P, P], F32, name="ident_f32")
-        make_identity(nc, ident_f32[:])
-
-        vectors = (b1, g1, be1, m1, v1, bfc1)
-        rows = const.tile([P, P], BF16, name="rows")
-        nc.vector.memset(rows[:], 0.0)
-        for v, vector in enumerate(vectors):
-            nc.scalar.dma_start(
-                out=rows[O_TILES * v : O_TILES * (v + 1), :],
-                in_=vector.rearrange("(r c) -> r c", c=P),
-            )
-        ft_sb = const.tile([P, C_OUT], BF16, name="ft_sb")
-        nc.scalar.dma_start(out=ft_sb[:], in_=ft)
-        wfc_sb = const.tile([P, O_TILES, C_OUT], BF16, name="wfc_sb")
-        nc.scalar.dma_start(out=wfc_sb[:], in_=Wfc1.rearrange("(t o) k -> o t k", o=P))
-
-        rows_t = tp_pool.tile([P, P], BF16, name="rows_t", tag="tp")
-        nc.tensor.transpose(rows_t[:], rows[:], ident_bf[:])
-        per_channel = const.tile([P, len(vectors), O_TILES], F32, name="per_channel")
-        nc.vector.tensor_copy(
-            out=per_channel[:].rearrange("p v o -> p (v o)"),
-            in_=rows_t[:, 0 : len(vectors) * O_TILES],
-        )
-        b1_c, g1_c, be1_c, m1_c, v1_c, bfc1_c = [
-            per_channel[:, v, :] for v in range(len(vectors))
-        ]
-
-        bn_scale = const.tile([P, O_TILES], F32, name="bn_scale")
-        bn_bias = const.tile([P, O_TILES], F32, name="bn_bias")
-        nc.vector.tensor_scalar_add(out=bn_scale[:], in0=v1_c, scalar1=EPS)
-        nc.scalar.sqrt(out=bn_scale[:], in_=bn_scale[:])
-        nc.vector.reciprocal(out=bn_scale[:], in_=bn_scale[:])
-        nc.vector.tensor_mul(out=bn_scale[:], in0=bn_scale[:], in1=g1_c)
-        nc.vector.tensor_sub(out=bn_bias[:], in0=b1_c, in1=m1_c)
-        nc.vector.tensor_mul(out=bn_bias[:], in0=bn_bias[:], in1=bn_scale[:])
-        nc.vector.tensor_add(out=bn_bias[:], in0=bn_bias[:], in1=be1_c)
-        gate_bias = const.tile([P, O_TILES], F32, name="gate_bias")
-        nc.vector.tensor_scalar_add(out=gate_bias[:], in0=bfc1_c, scalar1=1.0)
-
-        ft_t_ps = tp_pool.tile([P, K_TILES, P], BF16, name="ft_t_ps", tag="tp")
-        for kt in range(K_TILES):
-            nc.tensor.transpose(ft_t_ps[:, kt, :], ft_sb[:, kt * P : (kt + 1) * P], ident_bf[:])
-        ft_t = const.tile([P, K_TILES, P], BF16, name="ft_t")
-        nc.vector.tensor_copy(out=ft_t[:], in_=ft_t_ps[:])
-        wfc_t = const.tile([P, K_TILES, C_OUT], BF16, name="wfc_t")
-        for kt in range(K_TILES):
-            wfc_t_ps = tp_pool.tile([P, O_TILES, P], BF16, name="wfc_t_ps", tag="tp")
-            for ot in range(O_TILES):
-                nc.tensor.transpose(
-                    wfc_t_ps[:, ot, :], wfc_sb[:, ot, kt * P : (kt + 1) * P], ident_bf[:]
+            w_scales = const.tile([P, PASSES, C_OUT], U8, name="w_scales", align_bytes=64)
+            nc.vector.memset(w_scales[:].bitcast(I32), 0)
+            for quadrant in range(4):
+                nc.sync.dma_start(
+                    out=w_scales[32 * quadrant : 32 * quadrant + 4].bitcast(I32),
+                    in_=W1_scales[:, 4 * quadrant : 4 * quadrant + 4, :]
+                    .bitcast(I32)
+                    .rearrange("g r n -> r g n"),
                 )
+            steps = [
+                (chunk, g) for chunk in range(CHUNKS) for g in range(PASSES) if (chunk, g) not in TURNED
+            ]
+            raw_tiles = [load_chunk_pass(chunk, g) for chunk, g in steps[0:RAW_BUFS]]
+
+            ident_bf = const.tile([P, P], BF16, name="ident_bf")
+            make_identity(nc, ident_bf[:])
+            ident_f32 = const.tile([P, P], F32, name="ident_f32")
+            make_identity(nc, ident_f32[:])
+            to_slots = const.tile([P, P], F32, name="to_slots")
             nc.vector.tensor_copy(
-                out=wfc_t[:, kt, :], in_=wfc_t_ps[:].rearrange("p t o -> p (t o)")
+                out=to_slots[:].rearrange("p (k m r) -> p k m r", m=MEMBERS, r=OCTETS),
+                in_=ident_f32[:].rearrange("p (r m k) -> p k m r", m=MEMBERS, r=OCTETS),
             )
-        gate_t = const.tile([P, CHUNKS, MEMBERS, O_TILES, OCTETS], F32, name="gate_t")
-        for ot in range(O_TILES):
-            gate_t_ps = tp_pool.tile([P, B], F32, name="gate_t_ps", tag="tp")
+            bn_scale = const.tile([P, O_TILES], F32, name="bn_scale")
+            bn_bias = const.tile([P, O_TILES], F32, name="bn_bias")
+            gate = const.tile([P, CHUNKS, P], F32, name="gate")
+
+            rows_t = tp_pool.tile([P, P], BF16, name="rows_t", tag="tp")
+            nc.tensor.transpose(rows_t[:], rows[:], ident_bf[:])
+            per_channel = prep.tile([P, len(vectors), O_TILES], F32, name="per_channel")
+            nc.vector.tensor_copy(
+                out=per_channel[:].rearrange("p v o -> p (v o)"),
+                in_=rows_t[:, 0 : len(vectors) * O_TILES],
+            )
+            b1_c, g1_c, be1_c, m1_c, v1_c, bfc1_c = [
+                per_channel[:, v, :] for v in range(len(vectors))
+            ]
+
+            nc.vector.tensor_scalar_add(out=bn_scale[:], in0=v1_c, scalar1=EPS)
+            nc.scalar.sqrt(out=bn_scale[:], in_=bn_scale[:])
+            nc.vector.reciprocal(out=bn_scale[:], in_=bn_scale[:])
+            nc.vector.tensor_mul(out=bn_scale[:], in0=bn_scale[:], in1=g1_c)
+            nc.vector.tensor_sub(out=bn_bias[:], in0=b1_c, in1=m1_c)
+            nc.vector.tensor_mul(out=bn_bias[:], in0=bn_bias[:], in1=bn_scale[:])
+            nc.vector.tensor_add(out=bn_bias[:], in0=bn_bias[:], in1=be1_c)
+            gate_bias = prep.tile([P, O_TILES], F32, name="gate_bias")
+            nc.vector.tensor_scalar_add(out=gate_bias[:], in0=bfc1_c, scalar1=1.0)
+
+            ft_t_ps = tp_pool.tile([P, K_TILES, P], BF16, name="ft_t_ps", tag="tp")
             for kt in range(K_TILES):
-                nc.tensor.matmul(
-                    gate_t_ps[:],
-                    lhsT=wfc_t[:, kt, ot * P : (ot + 1) * P],
-                    rhs=ft_t[:, kt, :],
-                    start=(kt == 0),
-                    stop=(kt == K_TILES - 1),
+                nc.tensor.transpose(
+                    ft_t_ps[:, kt, :], ft_sb[:, kt * P : (kt + 1) * P], ident_bf[:]
                 )
-            nc.vector.tensor_scalar_add(
-                out=gate_t[:, :, :, ot, :],
-                in0=gate_t_ps[:].rearrange(
-                    "p (c r m) -> p c m r", r=OCTETS, m=MEMBERS
-                ),
-                scalar1=gate_bias[:, ot : ot + 1],
+            ft_t = prep.tile([P, K_TILES, P], BF16, name="ft_t")
+            nc.vector.tensor_copy(out=ft_t[:], in_=ft_t_ps[:])
+            wfc_t = prep.tile([P, K_TILES, C_OUT], BF16, name="wfc_t")
+            for kt in range(K_TILES):
+                wfc_t_ps = tp_pool.tile([P, O_TILES, P], BF16, name="wfc_t_ps", tag="tp")
+                for ot in range(O_TILES):
+                    nc.tensor.transpose(
+                        wfc_t_ps[:, ot, :], wfc_sb[:, ot, kt * P : (kt + 1) * P], ident_bf[:]
+                    )
+                nc.vector.tensor_copy(
+                    out=wfc_t[:, kt, :], in_=wfc_t_ps[:].rearrange("p t o -> p (t o)")
+                )
+            gate_t = prep.tile([P, CHUNKS, MEMBERS, O_TILES, OCTETS], F32, name="gate_t")
+            for ot in range(O_TILES):
+                gate_t_ps = tp_pool.tile([P, B], F32, name="gate_t_ps", tag="tp")
+                for kt in range(K_TILES):
+                    nc.tensor.matmul(
+                        gate_t_ps[:],
+                        lhsT=wfc_t[:, kt, ot * P : (ot + 1) * P],
+                        rhs=ft_t[:, kt, :],
+                        start=(kt == 0),
+                        stop=(kt == K_TILES - 1),
+                    )
+                nc.vector.tensor_scalar_add(
+                    out=gate_t[:, :, :, ot, :],
+                    in0=gate_t_ps[:].rearrange("p (c r m) -> p c m r", r=OCTETS, m=MEMBERS),
+                    scalar1=gate_bias[:, ot : ot + 1],
+                )
+            gate_ps = tp_pool.tile([P, CHUNKS, P], F32, name="gate_ps", tag="tp")
+            for chunk in range(CHUNKS):
+                nc.tensor.transpose(
+                    gate_ps[:, chunk, :],
+                    gate_t[:, chunk].rearrange("p m t r -> p (m t r)"),
+                    ident_f32[:],
+                )
+            nc.vector.tensor_copy(out=gate[:], in_=gate_ps[:])
+
+        fv1_pool = ctx.enter_context(tc.tile_pool(name="fv1", bufs=3))
+
+        turned_codes = const.tile(
+            [P, len(TURNED), CHUNK_COLS], U32, name="turned_codes", align_bytes=64
+        )
+        turned_scales = const.tile(
+            [P, len(TURNED), CHUNK_COLS], U8, name="turned_scales", align_bytes=64
+        )
+        by_word = whole[:].bitcast(F32).rearrange("b (p t j) -> b t j p", t=PACK, j=PIX // HALF)
+        grouped_pairs = {}
+
+        def turn_pair(pair):
+            grouped = grouped_pool.tile(
+                [P, len(TURNED), 2, NB, QUAD, PACK], BF16, name="grouped", align_bytes=64
             )
-        gate_ps = tp_pool.tile([P, CHUNKS, P], F32, name="gate_ps", tag="tp")
-        for chunk in range(CHUNKS):
-            nc.tensor.transpose(
-                gate_ps[:, chunk, :],
-                gate_t[:, chunk].rearrange("p m t r -> p (m t r)"),
-                ident_f32[:],
-            )
-        gate = const.tile([P, CHUNKS, P], F32, name="gate")
-        nc.vector.tensor_copy(out=gate[:], in_=gate_ps[:])
+            grouped_pairs[pair] = grouped
+            for u, q in enumerate(range(2 * pair, min(2 * pair + 2, QUADS))):
+                for half in range(QUAD // HALF):
+                    bank = tp_pool.tile([P, PACK, P], F32, name="turned", tag="tp")
+                    for t in range(PACK):
+                        nc.tensor.transpose(
+                            bank[:, t, :], by_word[:, t, q * (QUAD // HALF) + half, :], to_slots[:]
+                        )
+                    dst = grouped[:, :, u, :, half * HALF : (half + 1) * HALF, :]
+                    src = (
+                        bank[:]
+                        .rearrange("p t c -> p (t c)")
+                        .bitcast(BF16)
+                        .rearrange("p (t k s l) -> p k s l t", t=PACK, k=len(TURNED), l=HALF)
+                    )
+                    if pair < 2 and half == 1:
+                        nc.vector.tensor_copy(out=dst, in_=src)
+                    else:
+                        nc.scalar.copy(out=dst, in_=src)
+
+        def quantise_pair(pair):
+            grouped = grouped_pairs[pair]
+            units = min(2, QUADS - 2 * pair)
+            cols = slice(2 * pair * UNIT, (2 * pair + units) * UNIT)
+            for k in range(len(TURNED)):
+                nc.vector.quantize_mx(
+                    out=turned_codes[:, k, cols].bitcast(FP8X4),
+                    scales=turned_scales[:, k, cols],
+                    in_=grouped[:, k, 0:units].rearrange("p u s l t -> p (u s l t)"),
+                )
 
         mx_tiles = {}
         fv1_tiles = {}
         result_tiles = {}
 
-        def quantise_pass(chunk, g):
-            if g == 0:
+        def quantise_pass(chunk, g, vector_units):
+            if chunk not in mx_tiles:
                 mx_tiles[chunk] = (
                     mx_pool.tile([P, PASSES, CHUNK_COLS], U32, name="codes", align_bytes=64),
                     mx_pool.tile([P, PASSES, CHUNK_COLS], U8, name="scales", align_bytes=64),
                 )
             codes, scales = mx_tiles[chunk]
-            step = chunk * PASSES + g
+            step = steps.index((chunk, g))
             raw = raw_tiles[step]
-            if step + LOADS_AHEAD < len(steps):
-                raw_tiles.append(load_chunk_pass(*steps[step + LOADS_AHEAD]))
             grouped = grouped_pool.tile(
                 [P, QUADS, NB, QUAD, PACK], BF16, name="grouped", align_bytes=64
             )
             src = raw[:].rearrange("p s (t q l) -> p q s t l", t=PACK, l=QUAD)
             dst = grouped[:].rearrange("p q s l t -> p q s t l")
-            nc.vector.tensor_copy(out=dst[:, 0:VECTOR_UNITS], in_=src[:, 0:VECTOR_UNITS])
-            for q in range(VECTOR_UNITS, QUADS):
+            nc.vector.tensor_copy(out=dst[:, 0:vector_units], in_=src[:, 0:vector_units])
+            for q in range(vector_units, QUADS):
                 nc.scalar.copy(out=dst[:, q], in_=src[:, q])
+            if step + RAW_BUFS < len(steps):
+                raw_tiles.append(load_chunk_pass(*steps[step + RAW_BUFS]))
             for q0, nq in UNIT_GROUPS:
                 cols = slice(q0 * UNIT, (q0 + nq) * UNIT)
                 nc.vector.quantize_mx(
@@ -198,31 +261,30 @@ def tile_joint_module_pa_t_kernel(
                 )
 
         def convolve(chunk, group):
-            if group == 0:
-                fv1_tiles[chunk] = fv1_pool.tile(
-                    [P, PIX, MEMBERS, O_TILES, OCTETS], F32, name="fv1"
-                )
-            fv1 = fv1_tiles[chunk]
-            codes, scales = mx_tiles[chunk]
             q0, nq = UNIT_GROUPS[group]
+            fv1 = fv1_pool.tile([P, nq * QUAD, MEMBERS, O_TILES, OCTETS], F32, name="fv1")
+            fv1_tiles[(chunk, group)] = fv1
             cols = slice(q0 * UNIT, (q0 + nq) * UNIT)
             accs = [acc_pool.tile([P, 4 * UNIT], F32, name="acc") for ot in range(O_TILES)]
             for g in range(PASSES):
+                if (chunk, g) in TURNED:
+                    k = TURNED.index((chunk, g))
+                    rhs, rhs_scale = turned_codes[:, k, cols], turned_scales[:, k, cols]
+                else:
+                    rhs, rhs_scale = mx_tiles[chunk][0][:, g, cols], mx_tiles[chunk][1][:, g, cols]
                 for ot in range(O_TILES):
                     nc.tensor.matmul_mx(
                         out=accs[ot][:, 0 : nq * UNIT],
                         lhsT=w_words[:, g, 2 * P * ot : 2 * P * (ot + 1)].bitcast(FP4X4),
                         lhsT_scale=w_scales[:, g, P * ot : P * (ot + 1)],
-                        rhs=codes[:, g, cols].bitcast(FP8X4),
-                        rhs_scale=scales[:, g, cols],
+                        rhs=rhs.bitcast(FP8X4),
+                        rhs_scale=rhs_scale,
                         start=(g == 0),
                         stop=(g == PASSES - 1),
                     )
             for ot in range(O_TILES):
                 nc.scalar.activation(
-                    out=fv1[:, q0 * QUAD : (q0 + nq) * QUAD, :, ot, :].rearrange(
-                        "p (q l) m r -> p q l m r", l=QUAD
-                    ),
+                    out=fv1[:, :, :, ot, :].rearrange("p (q l) m r -> p q l m r", l=QUAD),
                     in_=accs[ot][:, 0 : nq * UNIT].rearrange(
                         "p (q m r l) -> p q l m r", m=MEMBERS, r=OCTETS, l=QUAD
                     ),
@@ -233,16 +295,18 @@ def tile_joint_module_pa_t_kernel(
 
         def flip(chunk, third):
             if third == 0:
-                result_tiles[chunk] = out_pool.tile([P, P, PIX], F32, name="result")
+                result_tiles[chunk] = big_pool.tile(
+                    [P, P, PIX], F32, name="result%d" % chunk, offset=((chunk + 2) % CHUNKS) * RESULT_BYTES
+                )
             result = result_tiles[chunk]
-            fv1 = fv1_tiles[chunk]
             gate_chunk = gate[:, chunk, :].unsqueeze(2).to_broadcast([P, P, QUAD])
             for q in range(third * QUADS // PASSES, (third + 1) * QUADS // PASSES):
+                fv1 = fv1_tiles[(chunk, q // 4)]
                 flipped = tp_pool.tile([P, QUAD, P], F32, name="flipped", tag="tp")
                 for lane in range(QUAD):
                     nc.tensor.transpose(
                         flipped[:, lane, :],
-                        fv1[:, q * QUAD + lane].rearrange("p m t r -> p (m t r)"),
+                        fv1[:, (q % 4) * QUAD + lane].rearrange("p m t r -> p (m t r)"),
                         ident_f32[:],
                     )
                 nc.vector.tensor_tensor(
@@ -252,26 +316,42 @@ def tile_joint_module_pa_t_kernel(
                     op=ALU.mult,
                 )
 
-        def quantise_next(chunk, g):
-            if chunk + 1 < CHUNKS:
-                quantise_pass(chunk + 1, g)
+        stored = []
 
-        for g in range(PASSES):
-            quantise_pass(0, g)
-        for chunk in range(CHUNKS):
-            for slot in range(PASSES):
-                quantise_next(chunk, slot)
-                convolve(chunk, slot)
-                if (chunk, slot) != (0, 0):
-                    flip(*divmod(chunk * PASSES + slot - 1, PASSES))
-        flip(CHUNKS - 1, PASSES - 1)
+        def store_finished(flips_done):
+            if len(raw_tiles) < len(steps):
+                return
+            for chunk in range(len(stored), flips_done // PASSES):
+                stored.append(chunk)
+                for octet in range(OCTETS):
+                    first = chunk * NB + octet * MEMBERS
+                    nc.sync.dma_start(
+                        out=out[first : first + MEMBERS].rearrange(
+                            "b (t o) h w -> (b t) (o h w)", t=O_TILES
+                        ),
+                        in_=result_tiles[chunk][octet:P:OCTETS].rearrange("p o x -> p (o x)"),
+                    )
 
-        for chunk in range(CHUNKS):
-            for octet in range(OCTETS):
-                first = chunk * NB + octet * MEMBERS
-                nc.sync.dma_start(
-                    out=out[first : first + MEMBERS].rearrange(
-                        "b (t o) h w -> (b t) (o h w)", t=O_TILES
-                    ),
-                    in_=result_tiles[chunk][octet:P:OCTETS].rearrange("p o x -> p (o x)"),
-                )
+        turn_pair(0)
+        turn_pair(1)
+        quantise_pair(0)
+        turn_pair(2)
+        quantise_pair(1)
+        quantise_pass(*steps[0], 8)
+        turn_pair(3)
+        quantise_pair(2)
+        convolve(0, 0)
+        turn_pair(4)
+        quantise_pair(3)
+        quantise_pass(*steps[1], 8)
+        convolve(0, 1)
+        flip(0, 0)
+        quantise_pair(4)
+        groups = CHUNKS * PASSES
+        for round_ in range(groups - 1):
+            if round_ + 2 < groups:
+                convolve(*divmod(round_ + 2, PASSES))
+            flip(*divmod(round_ + 1, PASSES))
+            if round_ + 2 < len(steps):
+                quantise_pass(*steps[round_ + 2], VECTOR_UNITS)
+            store_finished(round_ + 2)

@@ -347,11 +347,18 @@ def tile_joint_module_pa_t_kernel(
         convolve(0, 1)
         flip(0, 0)
         quantise_pair(4)
+        flip(0, 1)
         groups = CHUNKS * PASSES
-        for round_ in range(groups - 1):
-            if round_ + 2 < groups:
-                convolve(*divmod(round_ + 2, PASSES))
-            flip(*divmod(round_ + 1, PASSES))
-            if round_ + 2 < len(steps):
-                quantise_pass(*steps[round_ + 2], VECTOR_UNITS)
-            store_finished(round_ + 2)
+        for group in range(2, groups):
+            if group == groups - 1:
+                flip(*divmod(group - 1, PASSES))
+                convolve(*divmod(group, PASSES))
+            else:
+                convolve(*divmod(group, PASSES))
+                if group > 2:
+                    flip(*divmod(group - 1, PASSES))
+            if group < len(steps):
+                quantise_pass(*steps[group], VECTOR_UNITS if group < len(steps) - 2 else VECTOR_UNITS - 2)
+            store_finished(group)
+        flip(CHUNKS - 1, PASSES - 1)
+        store_finished(groups)

@@ -247,7 +247,12 @@ def tile_joint_module_pa_t_kernel(
             )
             src = raw[:].rearrange("p s (t q l) -> p q s t l", t=PACK, l=QUAD)
             dst = grouped[:].rearrange("p q s l t -> p q s t l")
-            nc.vector.tensor_copy(out=dst[:, 0:vector_units], in_=src[:, 0:vector_units])
+            first_units = UNIT_GROUPS[0][1]
+            nc.vector.tensor_copy(out=dst[:, 0:first_units], in_=src[:, 0:first_units])
+            if vector_units > first_units:
+                nc.vector.tensor_copy(
+                    out=dst[:, first_units:vector_units], in_=src[:, first_units:vector_units]
+                )
             for q in range(vector_units, QUADS):
                 nc.scalar.copy(out=dst[:, q], in_=src[:, q])
             if step + RAW_BUFS < len(steps):

@@ -213,7 +213,7 @@ def tile_joint_module_pa_t_kernel(
                         .bitcast(BF16)
                         .rearrange("p (t k s l) -> p k s l t", t=PACK, k=len(TURNED), l=HALF)
                     )
-                    if pair < 2 and half == 1:
+                    if half == 1 and (pair < 2 or (pair == 2 and u == 0)):
                         nc.vector.tensor_copy(out=dst, in_=src)
                     else:
                         nc.scalar.copy(out=dst, in_=src)

@@ -21,20 +21,20 @@ O_TILES = C_OUT // P
 K_TILES = C_OUT // P
 EPS = 1e-5
 
-OCTETS = 4
-MEMBERS = 8
-NB = OCTETS * MEMBERS
+NB = 32
 CHUNKS = B // NB
 QUAD = 4
 QUADS = PIX // QUAD
 UNIT = NB * QUAD
 CHUNK_COLS = QUADS * UNIT
+GROUPS = ((0, 512), (512, 512), (1024, 128))
 UNIT_GROUPS = ((0, 4), (4, 4), (8, 1))
-VECTOR_UNITS = 6
 RAW_BUFS = 4
 TURNED = ((0, 0), (0, 1), (0, 2), (1, 0))
-RESULT_BYTES = P * PIX * 4
 HALF = 2
+RESULT_BYTES = NB * O_TILES * PIX * 4
+RESULT_PLACES = (2, 3, 0, 2)
+BY_PIXEL = (0, 1)
 
 FLOPS = 2 * B * PIX * C_IN * C_OUT + 2 * B * C_OUT * C_OUT
 
@@ -49,18 +49,18 @@ def tile_joint_module_pa_t_kernel(
         big_pool = ctx.enter_context(tc.tile_pool(name="big", bufs=1))
         raw_pool = ctx.enter_context(tc.tile_pool(name="raw", bufs=RAW_BUFS))
         grouped_pool = ctx.enter_context(tc.tile_pool(name="grouped", bufs=3))
-        mx_pool = ctx.enter_context(tc.tile_pool(name="mx", bufs=2))
-        acc_pool = ctx.enter_context(tc.psum_pool(name="acc", bufs=4))
-        tp_pool = ctx.enter_context(tc.psum_pool(name="tp", bufs=4))
+        mx_pool = ctx.enter_context(tc.tile_pool(name="mx", bufs=3))
+        bank_pool = ctx.enter_context(tc.psum_pool(name="bank", bufs=8))
 
         def load_chunk_pass(chunk, g):
             raw = raw_pool.tile([P, NB, PACK * PIX], BF16, name="raw")
-            for octet in range(OCTETS):
-                first = chunk * NB + octet * MEMBERS
+            for part in range(4):
+                s0 = part * (NB // 4)
+                first = chunk * NB + s0
                 nc.sync.dma_start(
-                    out=raw[:, octet:NB:OCTETS, :],
+                    out=raw[:, s0 : s0 + NB // 4, :],
                     in_=fv[
-                        first : first + MEMBERS, g * P * PACK : (g + 1) * P * PACK, :, :
+                        first : first + NB // 4, g * P * PACK : (g + 1) * P * PACK, :, :
                     ].rearrange("b (p t) h w -> p b (t h w)", t=PACK),
                 )
             return raw
@@ -68,20 +68,18 @@ def tile_joint_module_pa_t_kernel(
         prep_pool = tc.tile_pool(name="prep", bufs=1)
         with prep_pool as prep:
             vectors = (b1, g1, be1, m1, v1, bfc1)
-            rows = prep.tile([P, P], BF16, name="rows")
-            nc.vector.memset(rows[:], 0.0)
+            per_channel = prep.tile([P, len(vectors), 16], BF16, name="per_channel")
             for v, vector in enumerate(vectors):
                 nc.sync.dma_start(
-                    out=rows[O_TILES * v : O_TILES * (v + 1), :],
-                    in_=vector.rearrange("(r c) -> r c", c=P),
+                    out=per_channel[:, v, 0:O_TILES],
+                    in_=vector.rearrange("(p t) -> p t", t=O_TILES),
                 )
             ft_sb = prep.tile([P, C_OUT], BF16, name="ft_sb")
             nc.sync.dma_start(out=ft_sb[:], in_=ft)
-            wfc_sb = prep.tile([P, O_TILES, C_OUT], BF16, name="wfc_sb")
-            nc.sync.dma_start(out=wfc_sb[:], in_=Wfc1.rearrange("(t o) k -> o t k", o=P))
-
             whole = big_pool.tile([P, P * PACK * PIX], BF16, name="whole", offset=0)
-            for k, (chunk, g) in enumerate(TURNED):
+
+            def load_turned(k):
+                chunk, g = TURNED[k]
                 nc.sync.dma_start(
                     out=whole[k : P : len(TURNED), :],
                     in_=fv[
@@ -89,19 +87,25 @@ def tile_joint_module_pa_t_kernel(
                     ].rearrange("b c h w -> b (c h w)"),
                 )
 
-            w_words = const.tile([P, PASSES, 2 * C_OUT], U8, name="w_words", align_bytes=64)
+            load_turned(0)
+            wfc_sb = prep.tile([P, O_TILES, C_OUT], BF16, name="wfc_sb")
+            nc.sync.dma_start(out=wfc_sb[:], in_=Wfc1.rearrange("(p t) k -> p t k", t=O_TILES))
+            w_raw = prep.tile([P, PASSES, 2 * C_OUT], U8, name="w_raw", align_bytes=64)
             nc.sync.dma_start(
-                out=w_words[:].bitcast(I32), in_=W1_words.bitcast(I32).rearrange("g p n -> p g n")
+                out=w_raw[:].bitcast(I32), in_=W1_words.bitcast(I32).rearrange("g p n -> p g n")
             )
-            w_scales = const.tile([P, PASSES, C_OUT], U8, name="w_scales", align_bytes=64)
-            nc.vector.memset(w_scales[:].bitcast(I32), 0)
+            s_raw = prep.tile([P, PASSES, C_OUT], U8, name="s_raw", align_bytes=64)
+            nc.vector.memset(s_raw[:].bitcast(I32), 0)
             for quadrant in range(4):
                 nc.sync.dma_start(
-                    out=w_scales[32 * quadrant : 32 * quadrant + 4].bitcast(I32),
+                    out=s_raw[32 * quadrant : 32 * quadrant + 4].bitcast(I32),
                     in_=W1_scales[:, 4 * quadrant : 4 * quadrant + 4, :]
                     .bitcast(I32)
                     .rearrange("g r n -> r g n"),
                 )
+            load_turned(1)
+            load_turned(2)
+            load_turned(3)
             steps = [
                 (chunk, g) for chunk in range(CHUNKS) for g in range(PASSES) if (chunk, g) not in TURNED
             ]
@@ -109,28 +113,19 @@ def tile_joint_module_pa_t_kernel(
 
             ident_bf = const.tile([P, P], BF16, name="ident_bf")
             make_identity(nc, ident_bf[:])
-            ident_f32 = const.tile([P, P], F32, name="ident_f32")
+            ident_f32 = prep.tile([P, P], F32, name="ident_f32")
             make_identity(nc, ident_f32[:])
             to_slots = const.tile([P, P], F32, name="to_slots")
             nc.vector.tensor_copy(
-                out=to_slots[:].rearrange("p (k m r) -> p k m r", m=MEMBERS, r=OCTETS),
-                in_=ident_f32[:].rearrange("p (r m k) -> p k m r", m=MEMBERS, r=OCTETS),
+                out=to_slots[:].rearrange("p (k b) -> p k b", b=NB),
+                in_=ident_f32[:].rearrange("p (b k) -> p k b", b=NB),
             )
             bn_scale = const.tile([P, O_TILES], F32, name="bn_scale")
             bn_bias = const.tile([P, O_TILES], F32, name="bn_bias")
-            gate = const.tile([P, CHUNKS, P], F32, name="gate")
-
-            rows_t = tp_pool.tile([P, P], BF16, name="rows_t", tag="tp")
-            nc.tensor.transpose(rows_t[:], rows[:], ident_bf[:])
-            per_channel = prep.tile([P, len(vectors), O_TILES], F32, name="per_channel")
-            nc.vector.tensor_copy(
-                out=per_channel[:].rearrange("p v o -> p (v o)"),
-                in_=rows_t[:, 0 : len(vectors) * O_TILES],
-            )
+            gate = const.tile([P, B, O_TILES], F32, name="gate")
             b1_c, g1_c, be1_c, m1_c, v1_c, bfc1_c = [
-                per_channel[:, v, :] for v in range(len(vectors))
+                per_channel[:, v, 0:O_TILES] for v in range(len(vectors))
             ]
-
             nc.vector.tensor_scalar_add(out=bn_scale[:], in0=v1_c, scalar1=EPS)
             nc.scalar.sqrt(out=bn_scale[:], in_=bn_scale[:])
             nc.vector.reciprocal(out=bn_scale[:], in_=bn_scale[:])
@@ -141,7 +136,7 @@ def tile_joint_module_pa_t_kernel(
             gate_bias = prep.tile([P, O_TILES], F32, name="gate_bias")
             nc.vector.tensor_scalar_add(out=gate_bias[:], in0=bfc1_c, scalar1=1.0)
 
-            ft_t_ps = tp_pool.tile([P, K_TILES, P], BF16, name="ft_t_ps", tag="tp")
+            ft_t_ps = bank_pool.tile([P, K_TILES, P], BF16, name="ft_t_ps", tag="bank")
             for kt in range(K_TILES):
                 nc.tensor.transpose(
                     ft_t_ps[:, kt, :], ft_sb[:, kt * P : (kt + 1) * P], ident_bf[:]
@@ -150,7 +145,7 @@ def tile_joint_module_pa_t_kernel(
             nc.vector.tensor_copy(out=ft_t[:], in_=ft_t_ps[:])
             wfc_t = prep.tile([P, K_TILES, C_OUT], BF16, name="wfc_t")
             for kt in range(K_TILES):
-                wfc_t_ps = tp_pool.tile([P, O_TILES, P], BF16, name="wfc_t_ps", tag="tp")
+                wfc_t_ps = bank_pool.tile([P, O_TILES, P], BF16, name="wfc_t_ps", tag="bank")
                 for ot in range(O_TILES):
                     nc.tensor.transpose(
                         wfc_t_ps[:, ot, :], wfc_sb[:, ot, kt * P : (kt + 1) * P], ident_bf[:]
@@ -158,41 +153,46 @@ def tile_joint_module_pa_t_kernel(
                 nc.vector.tensor_copy(
                     out=wfc_t[:, kt, :], in_=wfc_t_ps[:].rearrange("p t o -> p (t o)")
                 )
-            gate_t = prep.tile([P, CHUNKS, MEMBERS, O_TILES, OCTETS], F32, name="gate_t")
             for ot in range(O_TILES):
-                gate_t_ps = tp_pool.tile([P, B], F32, name="gate_t_ps", tag="tp")
+                gate_ps = bank_pool.tile([P, B], F32, name="gate_ps", tag="bank")
                 for kt in range(K_TILES):
                     nc.tensor.matmul(
-                        gate_t_ps[:],
+                        gate_ps[:],
                         lhsT=wfc_t[:, kt, ot * P : (ot + 1) * P],
                         rhs=ft_t[:, kt, :],
                         start=(kt == 0),
                         stop=(kt == K_TILES - 1),
                     )
                 nc.vector.tensor_scalar_add(
-                    out=gate_t[:, :, :, ot, :],
-                    in0=gate_t_ps[:].rearrange("p (c r m) -> p c m r", r=OCTETS, m=MEMBERS),
-                    scalar1=gate_bias[:, ot : ot + 1],
+                    out=gate[:, :, ot], in0=gate_ps[:], scalar1=gate_bias[:, ot : ot + 1]
                 )
-            gate_ps = tp_pool.tile([P, CHUNKS, P], F32, name="gate_ps", tag="tp")
-            for chunk in range(CHUNKS):
-                nc.tensor.transpose(
-                    gate_ps[:, chunk, :],
-                    gate_t[:, chunk].rearrange("p m t r -> p (m t r)"),
-                    ident_f32[:],
+            w_words = const.tile([P, PASSES, O_TILES, 2 * P], U8, name="w_words", align_bytes=64)
+            w_scales = const.tile([P, PASSES, O_TILES, P], U8, name="w_scales", align_bytes=64)
+            for g in range(PASSES):
+                nc.vector.tensor_copy(
+                    out=w_words[:, g].rearrange("p t (c b) -> p c t b", b=2),
+                    in_=w_raw[:, g].rearrange("p (c t b) -> p c t b", t=O_TILES, b=2),
                 )
-            nc.vector.tensor_copy(out=gate[:], in_=gate_ps[:])
+                nc.vector.tensor_copy(
+                    out=w_scales[:, g].rearrange("p t c -> p c t"),
+                    in_=s_raw[:, g].rearrange("p (c t) -> p c t", t=O_TILES),
+                )
 
-        fv1_pool = ctx.enter_context(tc.tile_pool(name="fv1", bufs=3))
+        fv1_pool = ctx.enter_context(tc.tile_pool(name="fv1", bufs=2))
 
-        turned_codes = const.tile(
-            [P, len(TURNED), CHUNK_COLS], U32, name="turned_codes", align_bytes=64
-        )
-        turned_scales = const.tile(
-            [P, len(TURNED), CHUNK_COLS], U8, name="turned_scales", align_bytes=64
-        )
         by_word = whole[:].bitcast(F32).rearrange("b (p t j) -> b t j p", t=PACK, j=PIX // HALF)
         grouped_pairs = {}
+        mx_tiles = {}
+        fv1_tiles = {}
+        result_tiles = {}
+
+        def mx_tile(chunk):
+            if chunk not in mx_tiles:
+                mx_tiles[chunk] = (
+                    mx_pool.tile([P, PASSES, CHUNK_COLS], U32, name="codes", align_bytes=64),
+                    mx_pool.tile([P, PASSES, CHUNK_COLS], U8, name="scales", align_bytes=64),
+                )
+            return mx_tiles[chunk]
 
         def turn_pair(pair):
             grouped = grouped_pool.tile(
@@ -201,7 +201,7 @@ def tile_joint_module_pa_t_kernel(
             grouped_pairs[pair] = grouped
             for u, q in enumerate(range(2 * pair, min(2 * pair + 2, QUADS))):
                 for half in range(QUAD // HALF):
-                    bank = tp_pool.tile([P, PACK, P], F32, name="turned", tag="tp")
+                    bank = bank_pool.tile([P, PACK, P], F32, name="turned", tag="bank")
                     for t in range(PACK):
                         nc.tensor.transpose(
                             bank[:, t, :], by_word[:, t, q * (QUAD // HALF) + half, :], to_slots[:]
@@ -222,148 +222,171 @@ def tile_joint_module_pa_t_kernel(
             grouped = grouped_pairs[pair]
             units = min(2, QUADS - 2 * pair)
             cols = slice(2 * pair * UNIT, (2 * pair + units) * UNIT)
-            for k in range(len(TURNED)):
-                nc.vector.quantize_mx(
-                    out=turned_codes[:, k, cols].bitcast(FP8X4),
-                    scales=turned_scales[:, k, cols],
-                    in_=grouped[:, k, 0:units].rearrange("p u s l t -> p (u s l t)"),
-                )
-
-        mx_tiles = {}
-        fv1_tiles = {}
-        result_tiles = {}
-
-        def quantise_pass(chunk, g, vector_units):
-            if chunk not in mx_tiles:
-                mx_tiles[chunk] = (
-                    mx_pool.tile([P, PASSES, CHUNK_COLS], U32, name="codes", align_bytes=64),
-                    mx_pool.tile([P, PASSES, CHUNK_COLS], U8, name="scales", align_bytes=64),
-                )
-            codes, scales = mx_tiles[chunk]
-            step = steps.index((chunk, g))
-            raw = raw_tiles[step]
-            grouped = grouped_pool.tile(
-                [P, QUADS, NB, QUAD, PACK], BF16, name="grouped", align_bytes=64
-            )
-            src = raw[:].rearrange("p s (t q l) -> p q s t l", t=PACK, l=QUAD)
-            dst = grouped[:].rearrange("p q s l t -> p q s t l")
-            first_units = UNIT_GROUPS[0][1]
-            nc.vector.tensor_copy(out=dst[:, 0:first_units], in_=src[:, 0:first_units])
-            if vector_units > first_units:
-                nc.vector.tensor_copy(
-                    out=dst[:, first_units:vector_units], in_=src[:, first_units:vector_units]
-                )
-            for q in range(vector_units, QUADS):
-                nc.scalar.copy(out=dst[:, q], in_=src[:, q])
-            if step + RAW_BUFS < len(steps):
-                raw_tiles.append(load_chunk_pass(*steps[step + RAW_BUFS]))
-            for q0, nq in UNIT_GROUPS:
-                cols = slice(q0 * UNIT, (q0 + nq) * UNIT)
+            for k, (chunk, g) in enumerate(TURNED):
+                codes, scales = mx_tile(chunk)
                 nc.vector.quantize_mx(
                     out=codes[:, g, cols].bitcast(FP8X4),
                     scales=scales[:, g, cols],
-                    in_=grouped[:, q0 : q0 + nq].rearrange("p q s l t -> p (q s l t)"),
+                    in_=grouped[:, k, 0:units].rearrange("p u s l t -> p (u s l t)"),
+                )
+
+        def quantise_pass(chunk, g, vector_cuts, scalar_cuts):
+            codes, scales = mx_tile(chunk)
+            step = steps.index((chunk, g))
+            raw = raw_tiles[step]
+            if chunk in BY_PIXEL:
+                grouped = grouped_pool.tile(
+                    [P, QUADS, NB, QUAD, PACK], BF16, name="grouped", align_bytes=64
+                )
+                src = raw[:].rearrange("p s (t q l) -> p q s t l", t=PACK, l=QUAD)
+                dst = grouped[:].rearrange("p q s l t -> p q s t l")
+                flat = grouped[:].rearrange("p q s l t -> p (q s l t)")
+            else:
+                grouped = grouped_pool.tile(
+                    [P, NB, QUADS, QUAD, PACK], BF16, name="grouped", align_bytes=64
+                )
+                src = raw[:].rearrange("p s (t q l) -> p s q t l", t=PACK, l=QUAD)
+                dst = grouped[:].rearrange("p s q l t -> p s q t l")
+                flat = grouped[:].rearrange("p s q l t -> p (s q l t)")
+            for a, b in zip(vector_cuts, vector_cuts[1:]):
+                nc.vector.tensor_copy(out=dst[:, a:b], in_=src[:, a:b])
+            for a, b in zip(scalar_cuts, scalar_cuts[1:]):
+                nc.scalar.copy(out=dst[:, a:b], in_=src[:, a:b])
+            if step + RAW_BUFS < len(steps):
+                raw_tiles.append(load_chunk_pass(*steps[step + RAW_BUFS]))
+            for c0, n in GROUPS:
+                nc.vector.quantize_mx(
+                    out=codes[:, g, c0 : c0 + n].bitcast(FP8X4),
+                    scales=scales[:, g, c0 : c0 + n],
+                    in_=flat[:, PACK * c0 : PACK * (c0 + n)],
                 )
 
         def convolve(chunk, group):
+            codes, scales = mx_tiles[chunk]
+            c0, n = GROUPS[group]
             q0, nq = UNIT_GROUPS[group]
-            fv1 = fv1_pool.tile([P, nq * QUAD, MEMBERS, O_TILES, OCTETS], F32, name="fv1")
-            fv1_tiles[(chunk, group)] = fv1
-            cols = slice(q0 * UNIT, (q0 + nq) * UNIT)
-            accs = [acc_pool.tile([P, 4 * UNIT], F32, name="acc") for ot in range(O_TILES)]
-            for g in range(PASSES):
-                if (chunk, g) in TURNED:
-                    k = TURNED.index((chunk, g))
-                    rhs, rhs_scale = turned_codes[:, k, cols], turned_scales[:, k, cols]
+            cols = slice(c0, c0 + n)
+            if chunk in BY_PIXEL:
+                fv1 = fv1_pool.tile([P, O_TILES, NB, nq * QUAD], F32, name="fv1p%d" % group, bufs=1)
+                fv1_tiles[(chunk, group)] = fv1
+            elif group == 0:
+                if chunk == CHUNKS - 1:
+                    fv1 = big_pool.tile(
+                        [P, O_TILES, CHUNK_COLS], F32, name="fv1_last", offset=RESULT_BYTES
+                    )
                 else:
-                    rhs, rhs_scale = mx_tiles[chunk][0][:, g, cols], mx_tiles[chunk][1][:, g, cols]
+                    fv1 = fv1_pool.tile([P, O_TILES, CHUNK_COLS], F32, name="fv1", bufs=1)
+                fv1_tiles[chunk] = fv1
+            else:
+                fv1 = fv1_tiles[chunk]
+            accs = [bank_pool.tile([P, 512], F32, name="acc", tag="bank") for ot in range(O_TILES)]
+            for g in range(PASSES):
                 for ot in range(O_TILES):
                     nc.tensor.matmul_mx(
-                        out=accs[ot][:, 0 : nq * UNIT],
-                        lhsT=w_words[:, g, 2 * P * ot : 2 * P * (ot + 1)].bitcast(FP4X4),
-                        lhsT_scale=w_scales[:, g, P * ot : P * (ot + 1)],
-                        rhs=rhs.bitcast(FP8X4),
-                        rhs_scale=rhs_scale,
+                        out=accs[ot][:, 0:n],
+                        lhsT=w_words[:, g, ot].bitcast(FP4X4),
+                        lhsT_scale=w_scales[:, g, ot],
+                        rhs=codes[:, g, cols].bitcast(FP8X4),
+                        rhs_scale=scales[:, g, cols],
                         start=(g == 0),
                         stop=(g == PASSES - 1),
                     )
             for ot in range(O_TILES):
+                if chunk in BY_PIXEL:
+                    dst = fv1[:, ot].rearrange("p s (q l) -> p q s l", l=QUAD)
+                    src = accs[ot][:, 0:n].rearrange("p (q s l) -> p q s l", s=NB, l=QUAD)
+                else:
+                    dst = fv1[:, ot, cols]
+                    src = accs[ot][:, 0:n]
                 nc.scalar.activation(
-                    out=fv1[:, :, :, ot, :].rearrange("p (q l) m r -> p q l m r", l=QUAD),
-                    in_=accs[ot][:, 0 : nq * UNIT].rearrange(
-                        "p (q m r l) -> p q l m r", m=MEMBERS, r=OCTETS, l=QUAD
-                    ),
+                    out=dst,
+                    in_=src,
                     func=ACT.Relu,
                     scale=bn_scale[:, ot : ot + 1],
                     bias=bn_bias[:, ot : ot + 1],
                 )
 
-        def flip(chunk, third):
-            if third == 0:
+        def multiply(chunk, group):
+            if group == 0:
                 result_tiles[chunk] = big_pool.tile(
-                    [P, P, PIX], F32, name="result%d" % chunk, offset=((chunk + 2) % CHUNKS) * RESULT_BYTES
+                    [P, NB, O_TILES, PIX], F32, name="result%d" % chunk,
+                    offset=RESULT_PLACES[chunk] * RESULT_BYTES,
                 )
             result = result_tiles[chunk]
-            gate_chunk = gate[:, chunk, :].unsqueeze(2).to_broadcast([P, P, QUAD])
-            for q in range(third * QUADS // PASSES, (third + 1) * QUADS // PASSES):
-                fv1 = fv1_tiles[(chunk, q // 4)]
-                flipped = tp_pool.tile([P, QUAD, P], F32, name="flipped", tag="tp")
-                for lane in range(QUAD):
-                    nc.tensor.transpose(
-                        flipped[:, lane, :],
-                        fv1[:, (q % 4) * QUAD + lane].rearrange("p m t r -> p (m t r)"),
-                        ident_f32[:],
-                    )
-                nc.vector.tensor_tensor(
-                    out=result[:, :, q * QUAD : (q + 1) * QUAD],
-                    in0=flipped[:].rearrange("p l o -> p o l"),
-                    in1=gate_chunk,
-                    op=ALU.mult,
-                )
+            if chunk in BY_PIXEL:
+                q0, nq = UNIT_GROUPS[group]
+                samples = slice(0, NB)
+                pixels = slice(q0 * QUAD, (q0 + nq) * QUAD)
+                in0 = fv1_tiles[(chunk, group)][:].rearrange("p t s x -> p s t x")
+            else:
+                c0, n = GROUPS[group]
+                samples = slice(c0 // PIX, (c0 + n) // PIX)
+                pixels = slice(0, PIX)
+                in0 = fv1_tiles[chunk][:].rearrange("p t (s x) -> p s t x", x=PIX)[:, samples]
+            ns = samples.stop - samples.start
+            gate_bc = (
+                gate[:, chunk * NB + samples.start : chunk * NB + samples.stop, :]
+                .unsqueeze(3)
+                .to_broadcast([P, ns, O_TILES, pixels.stop - pixels.start])
+            )
+            nc.vector.tensor_tensor(
+                out=result[:, samples, :, pixels], in0=in0, in1=gate_bc, op=ALU.mult
+            )
 
-        stored = []
+        def store(chunk, s0, s1):
+            first = chunk * NB
+            nc.sync.dma_start(
+                out=out[first + s0 : first + s1].rearrange(
+                    "b (p t) h w -> p b (t h w)", t=O_TILES
+                ),
+                in_=result_tiles[chunk][:, s0:s1].rearrange("p s t x -> p s (t x)"),
+            )
 
-        def store_finished(flips_done):
-            if len(raw_tiles) < len(steps):
-                return
-            for chunk in range(len(stored), flips_done // PASSES):
-                stored.append(chunk)
-                for octet in range(OCTETS):
-                    first = chunk * NB + octet * MEMBERS
-                    nc.sync.dma_start(
-                        out=out[first : first + MEMBERS].rearrange(
-                            "b (t o) h w -> (b t) (o h w)", t=O_TILES
-                        ),
-                        in_=result_tiles[chunk][octet:P:OCTETS].rearrange("p o x -> p (o x)"),
-                    )
+        def store_chunk(chunk, group):
+            if chunk in BY_PIXEL:
+                if group == PASSES - 1:
+                    for s0 in range(0, NB, 8):
+                        store(chunk, s0, s0 + 8)
+            else:
+                c0, n = GROUPS[group]
+                a, b = c0 // PIX, (c0 + n) // PIX
+                if b - a > 8:
+                    store(chunk, a, (a + b) // 2)
+                    store(chunk, (a + b) // 2, b)
+                else:
+                    store(chunk, a, b)
 
+        pix = lambda n: ((0, 4, n) if n > 4 else (0, 4), tuple(range(n, QUADS + 1)))
+        smp = lambda n: ((0, 16, n) if n > 16 else (0, 16), (n, 29, 32))
         turn_pair(0)
         turn_pair(1)
         quantise_pair(0)
         turn_pair(2)
         quantise_pair(1)
-        quantise_pass(*steps[0], 8)
+        quantise_pass(*steps[0], *pix(8))
         turn_pair(3)
         quantise_pair(2)
         convolve(0, 0)
         turn_pair(4)
         quantise_pair(3)
-        quantise_pass(*steps[1], 8)
+        quantise_pass(*steps[1], *pix(8))
         convolve(0, 1)
-        flip(0, 0)
+        multiply(0, 0)
         quantise_pair(4)
-        flip(0, 1)
-        groups = CHUNKS * PASSES
-        for group in range(2, groups):
-            if group == groups - 1:
-                flip(*divmod(group - 1, PASSES))
-                convolve(*divmod(group, PASSES))
-            else:
-                convolve(*divmod(group, PASSES))
-                if group > 2:
-                    flip(*divmod(group - 1, PASSES))
-            if group < len(steps):
-                quantise_pass(*steps[group], VECTOR_UNITS if group < len(steps) - 2 else VECTOR_UNITS - 2)
-            store_finished(group)
-        flip(CHUNKS - 1, PASSES - 1)
-        store_finished(groups)
+        convolve(0, 2)
+        multiply(0, 1)
+
+        quantise_pass(*steps[2], *smp(18))
+        convolve(1, 0)
+        multiply(0, 2)
+        for i in range(3, 11):
+            if i < len(steps):
+                quantise_pass(*steps[i], *smp(16))
+            convolve(*divmod(i + 1, 3))
+            multiply(*divmod(i, 3))
+
+        multiply(3, 2)
+
+        for chunk in range(CHUNKS):
+            for group in range(3):
+                store_chunk(chunk, group)

@@ -32,6 +32,7 @@ UNIT_GROUPS = ((0, 4), (4, 4), (8, 1))
 RAW_BUFS = 4
 TURNED = ((0, 0), (0, 1), (0, 2), (1, 0))
 HALF = 2
+SAMPLE_CUTS = ((0, 14), (14, 28), (28, 32), (14, 21), (21, 28))
 RESULT_BYTES = NB * O_TILES * PIX * 4
 RESULT_PLACES = (2, 3, 0, 2)
 BY_PIXEL = (0, 1)
@@ -230,9 +231,10 @@ def tile_joint_module_pa_t_kernel(
                     in_=grouped[:, k, 0:units].rearrange("p u s l t -> p (u s l t)"),
                 )
 
-        def quantise_pass(chunk, g, vector_cuts, scalar_cuts):
-            codes, scales = mx_tile(chunk)
-            step = steps.index((chunk, g))
+        flat_tiles = {}
+
+        def regroup(step, vector_cuts, scalar_cuts):
+            chunk, g = steps[step]
             raw = raw_tiles[step]
             if chunk in BY_PIXEL:
                 grouped = grouped_pool.tile(
@@ -254,11 +256,16 @@ def tile_joint_module_pa_t_kernel(
                 nc.scalar.copy(out=dst[:, a:b], in_=src[:, a:b])
             if step + RAW_BUFS < len(steps):
                 raw_tiles.append(load_chunk_pass(*steps[step + RAW_BUFS]))
+            flat_tiles[step] = flat
+
+        def quantise(step):
+            chunk, g = steps[step]
+            codes, scales = mx_tile(chunk)
             for c0, n in GROUPS:
                 nc.vector.quantize_mx(
                     out=codes[:, g, c0 : c0 + n].bitcast(FP8X4),
                     scales=scales[:, g, c0 : c0 + n],
-                    in_=flat[:, PACK * c0 : PACK * (c0 + n)],
+                    in_=flat_tiles[step][:, PACK * c0 : PACK * (c0 + n)],
                 )
 
         def convolve(chunk, group):
@@ -319,8 +326,7 @@ def tile_joint_module_pa_t_kernel(
                 pixels = slice(q0 * QUAD, (q0 + nq) * QUAD)
                 in0 = fv1_tiles[(chunk, group)][:].rearrange("p t s x -> p s t x")
             else:
-                c0, n = GROUPS[group]
-                samples = slice(c0 // PIX, (c0 + n) // PIX)
+                samples = slice(*SAMPLE_CUTS[group])
                 pixels = slice(0, PIX)
                 in0 = fv1_tiles[chunk][:].rearrange("p t (s x) -> p s t x", x=PIX)[:, samples]
             ns = samples.stop - samples.start
@@ -348,45 +354,62 @@ def tile_joint_module_pa_t_kernel(
                     for s0 in range(0, NB, 8):
                         store(chunk, s0, s0 + 8)
             else:
-                c0, n = GROUPS[group]
-                a, b = c0 // PIX, (c0 + n) // PIX
+                a, b = SAMPLE_CUTS[group]
                 if b - a > 8:
                     store(chunk, a, (a + b) // 2)
                     store(chunk, (a + b) // 2, b)
                 else:
                     store(chunk, a, b)
 
+        finished = []
+
+        def finish(chunk, group):
+            multiply(chunk, group)
+            finished.append((chunk, group))
+            if len(raw_tiles) == len(steps):
+                for pair in finished:
+                    store_chunk(*pair)
+                finished.clear()
+
         pix = lambda n: ((0, 4, n) if n > 4 else (0, 4), tuple(range(n, QUADS + 1)))
-        smp = lambda n: ((0, 16, n) if n > 16 else (0, 16), (n, 29, 32))
+        smp = lambda n: ((0, 16, n) if n > 16 else (0, n), (n, 29, 32))
         turn_pair(0)
         turn_pair(1)
         quantise_pair(0)
         turn_pair(2)
         quantise_pair(1)
-        quantise_pass(*steps[0], *pix(8))
+        regroup(0, *pix(8))
+        quantise(0)
         turn_pair(3)
         quantise_pair(2)
         convolve(0, 0)
         turn_pair(4)
         quantise_pair(3)
-        quantise_pass(*steps[1], *pix(8))
+        regroup(1, *pix(8))
+        quantise(1)
         convolve(0, 1)
-        multiply(0, 0)
+        finish(0, 0)
         quantise_pair(4)
         convolve(0, 2)
-        multiply(0, 1)
-
-        quantise_pass(*steps[2], *smp(18))
+        regroup(2, *smp(18))
+        finish(0, 1)
+        quantise(2)
         convolve(1, 0)
-        multiply(0, 2)
-        for i in range(3, 11):
-            if i < len(steps):
-                quantise_pass(*steps[i], *smp(16))
-            convolve(*divmod(i + 1, 3))
-            multiply(*divmod(i, 3))
-
-        multiply(3, 2)
-
-        for chunk in range(CHUNKS):
-            for group in range(3):
-                store_chunk(chunk, group)
+        regroup(3, *smp(16))
+        finish(0, 2)
+        quantise(3)
+        for i in range(4, 8):
+            convolve(*divmod(i, 3))
+            regroup(i, *smp(16))
+            finish(*divmod(i - 1, 3))
+            quantise(i)
+        convolve(2, 2)
+        finish(2, 1)
+        convolve(3, 0)
+        finish(2, 2)
+        convolve(3, 1)
+        finish(3, 0)
+        convolve(3, 2)
+        finish(3, 3)
+        finish(3, 4)
+        finish(3, 2)

@@ -30,6 +30,7 @@ CHUNK_COLS = QUADS * UNIT
 GROUPS = ((0, 512), (512, 512), (1024, 128))
 UNIT_GROUPS = ((0, 4), (4, 4), (8, 1))
 RAW_BUFS = 4
+LOAD_PARTS = 1
 TURNED = ((0, 0), (0, 1), (0, 2), (1, 0))
 HALF = 2
 SAMPLE_CUTS = ((0, 14), (14, 28), (28, 32), (14, 21), (21, 28))
@@ -55,13 +56,13 @@ def tile_joint_module_pa_t_kernel(
 
         def load_chunk_pass(chunk, g):
             raw = raw_pool.tile([P, NB, PACK * PIX], BF16, name="raw")
-            for part in range(4):
-                s0 = part * (NB // 4)
+            for part in range(LOAD_PARTS):
+                s0 = part * (NB // LOAD_PARTS)
                 first = chunk * NB + s0
                 nc.sync.dma_start(
-                    out=raw[:, s0 : s0 + NB // 4, :],
+                    out=raw[:, s0 : s0 + NB // LOAD_PARTS, :],
                     in_=fv[
-                        first : first + NB // 4, g * P * PACK : (g + 1) * P * PACK, :, :
+                        first : first + NB // LOAD_PARTS, g * P * PACK : (g + 1) * P * PACK, :, :
                     ].rearrange("b (p t) h w -> p b (t h w)", t=PACK),
                 )
             return raw
@@ -351,8 +352,8 @@ def tile_joint_module_pa_t_kernel(
         def store_chunk(chunk, group):
             if chunk in BY_PIXEL:
                 if group == PASSES - 1:
-                    for s0 in range(0, NB, 8):
-                        store(chunk, s0, s0 + 8)
+                    for s0 in range(0, NB, 16):
+                        store(chunk, s0, s0 + 16)
             else:
                 a, b = SAMPLE_CUTS[group]
                 if b - a > 8:

@@ -124,7 +124,7 @@ def tile_joint_module_pa_t_kernel(
             )
             bn_scale = const.tile([P, O_TILES], F32, name="bn_scale")
             bn_bias = const.tile([P, O_TILES], F32, name="bn_bias")
-            gate = const.tile([P, B, O_TILES], F32, name="gate")
+            gate = const.tile([P, O_TILES, B], F32, name="gate")
             b1_c, g1_c, be1_c, m1_c, v1_c, bfc1_c = [
                 per_channel[:, v, 0:O_TILES] for v in range(len(vectors))
             ]
@@ -166,18 +166,18 @@ def tile_joint_module_pa_t_kernel(
                         stop=(kt == K_TILES - 1),
                     )
                 nc.vector.tensor_scalar_add(
-                    out=gate[:, :, ot], in0=gate_ps[:], scalar1=gate_bias[:, ot : ot + 1]
+                    out=gate[:, ot, :], in0=gate_ps[:], scalar1=gate_bias[:, ot : ot + 1]
                 )
             w_words = const.tile([P, PASSES, O_TILES, 2 * P], U8, name="w_words", align_bytes=64)
             w_scales = const.tile([P, PASSES, O_TILES, P], U8, name="w_scales", align_bytes=64)
             for g in range(PASSES):
                 nc.vector.tensor_copy(
-                    out=w_words[:, g].rearrange("p t (c b) -> p c t b", b=2),
-                    in_=w_raw[:, g].rearrange("p (c t b) -> p c t b", t=O_TILES, b=2),
+                    out=w_words[:, g].rearrange("p t (c b) -> p t c b", b=2),
+                    in_=w_raw[:, g].rearrange("p (c t b) -> p t c b", t=O_TILES, b=2),
                 )
-                nc.vector.tensor_copy(
-                    out=w_scales[:, g].rearrange("p t c -> p c t"),
-                    in_=s_raw[:, g].rearrange("p (c t) -> p c t", t=O_TILES),
+                nc.gpsimd.tensor_copy(
+                    out=w_scales[:, g],
+                    in_=s_raw[:, g].rearrange("p (c t) -> p t c", t=O_TILES),
                 )
 
         fv1_pool = ctx.enter_context(tc.tile_pool(name="fv1", bufs=2))
@@ -332,7 +332,8 @@ def tile_joint_module_pa_t_kernel(
                 in0 = fv1_tiles[chunk][:].rearrange("p t (s x) -> p s t x", x=PIX)[:, samples]
             ns = samples.stop - samples.start
             gate_bc = (
-                gate[:, chunk * NB + samples.start : chunk * NB + samples.stop, :]
+                gate[:, :, chunk * NB + samples.start : chunk * NB + samples.stop]
+                .rearrange("p t s -> p s t")
                 .unsqueeze(3)
                 .to_broadcast([P, ns, O_TILES, pixels.stop - pixels.start])
             )

@@ -69,15 +69,6 @@ def tile_joint_module_pa_t_kernel(
 
         prep_pool = tc.tile_pool(name="prep", bufs=1)
         with prep_pool as prep:
-            vectors = (b1, g1, be1, m1, v1, bfc1)
-            per_channel = prep.tile([P, len(vectors), 16], BF16, name="per_channel")
-            for v, vector in enumerate(vectors):
-                nc.sync.dma_start(
-                    out=per_channel[:, v, 0:O_TILES],
-                    in_=vector.rearrange("(p t) -> p t", t=O_TILES),
-                )
-            ft_sb = prep.tile([P, C_OUT], BF16, name="ft_sb")
-            nc.sync.dma_start(out=ft_sb[:], in_=ft)
             whole = big_pool.tile([P, P * PACK * PIX], BF16, name="whole", offset=0)
 
             def load_turned(k):
@@ -89,7 +80,15 @@ def tile_joint_module_pa_t_kernel(
                     ].rearrange("b c h w -> b (c h w)"),
                 )
 
-            load_turned(0)
+            vectors = (b1, g1, be1, m1, v1, bfc1)
+            rows = prep.tile([P, C_OUT], BF16, name="rows")
+            nc.gpsimd.memset(rows[:].bitcast(F32), 0.0)
+            for v, vector in enumerate(vectors):
+                if v % 3 == 0:
+                    load_turned(v // 3)
+                nc.sync.dma_start(out=rows[v : v + 1, :], in_=vector.rearrange("(r c) -> r c", r=1))
+            ft_sb = prep.tile([P, C_OUT], BF16, name="ft_sb")
+            nc.sync.dma_start(out=ft_sb[:], in_=ft)
             wfc_sb = prep.tile([P, O_TILES, C_OUT], BF16, name="wfc_sb")
             nc.sync.dma_start(out=wfc_sb[:], in_=Wfc1.rearrange("(p t) k -> p t k", t=O_TILES))
             w_raw = prep.tile([P, PASSES, 2 * C_OUT], U8, name="w_raw", align_bytes=64)
@@ -98,14 +97,11 @@ def tile_joint_module_pa_t_kernel(
             )
             s_raw = prep.tile([P, PASSES, C_OUT], U8, name="s_raw", align_bytes=64)
             nc.vector.memset(s_raw[:].bitcast(I32), 0)
-            for quadrant in range(4):
+            for row in range(4):
                 nc.sync.dma_start(
-                    out=s_raw[32 * quadrant : 32 * quadrant + 4].bitcast(I32),
-                    in_=W1_scales[:, 4 * quadrant : 4 * quadrant + 4, :]
-                    .bitcast(I32)
-                    .rearrange("g r n -> r g n"),
+                    out=s_raw[row : P : 32].bitcast(I32),
+                    in_=W1_scales[:, row:16:4, :].bitcast(I32).rearrange("g q n -> q g n"),
                 )
-            load_turned(1)
             load_turned(2)
             load_turned(3)
             steps = [
@@ -125,8 +121,15 @@ def tile_joint_module_pa_t_kernel(
             bn_scale = const.tile([P, O_TILES], F32, name="bn_scale")
             bn_bias = const.tile([P, O_TILES], F32, name="bn_bias")
             gate = const.tile([P, O_TILES, B], F32, name="gate")
+            rows_t = bank_pool.tile([P, O_TILES, P], BF16, name="rows_t", tag="bank")
+            for ot in range(O_TILES):
+                nc.tensor.transpose(rows_t[:, ot, :], rows[:, ot:C_OUT:O_TILES], ident_bf[:])
+            per_channel = prep.tile([P, len(vectors), O_TILES], F32, name="per_channel")
+            nc.vector.tensor_copy(
+                out=per_channel[:].rearrange("p v t -> p t v"), in_=rows_t[:, :, 0 : len(vectors)]
+            )
             b1_c, g1_c, be1_c, m1_c, v1_c, bfc1_c = [
-                per_channel[:, v, 0:O_TILES] for v in range(len(vectors))
+                per_channel[:, v, :] for v in range(len(vectors))
             ]
             nc.vector.tensor_scalar_add(out=bn_scale[:], in0=v1_c, scalar1=EPS)
             nc.scalar.sqrt(out=bn_scale[:], in_=bn_scale[:])
@@ -353,15 +356,10 @@ def tile_joint_module_pa_t_kernel(
         def store_chunk(chunk, group):
             if chunk in BY_PIXEL:
                 if group == PASSES - 1:
-                    for s0 in range(0, NB, 16):
-                        store(chunk, s0, s0 + 16)
+                    store(chunk, 0, NB)
             else:
                 a, b = SAMPLE_CUTS[group]
-                if b - a > 8:
-                    store(chunk, a, (a + b) // 2)
-                    store(chunk, (a + b) // 2, b)
-                else:
-                    store(chunk, a, b)
+                store(chunk, a, b)
 
         finished = []
 
@@ -374,7 +372,7 @@ def tile_joint_module_pa_t_kernel(
                 finished.clear()
 
         pix = lambda n: ((0, 4, n) if n > 4 else (0, 4), tuple(range(n, QUADS + 1)))
-        smp = lambda n: ((0, 16, n) if n > 16 else (0, n), (n, 29, 32))
+        smp = lambda n: ((0, n), (n, 29, 32))
         turn_pair(0)
         turn_pair(1)
         quantise_pair(0)

from contextlib import ExitStack

import concourse.mybir as mybir
from concourse.masks import make_identity

BF16 = mybir.dt.bfloat16
F32 = mybir.dt.float32
I32 = mybir.dt.int32
U8 = mybir.dt.uint8
U32 = mybir.dt.uint32
FP8X4 = mybir.dt.float8_e4m3fn_x4
FP4X4 = mybir.dt.float4_e2m1fn_x4
ACT = mybir.ActivationFunctionType
ALU = mybir.AluOpType

P = 128
PACK = 4
B, C_IN, C_OUT, PIX = 128, 1536, 512, 36
PASSES = C_IN // (P * PACK)
O_TILES = C_OUT // P
K_TILES = C_OUT // P
EPS = 1e-5

NB = 32
CHUNKS = B // NB
QUAD = 4
QUADS = PIX // QUAD
UNIT = NB * QUAD
CHUNK_COLS = QUADS * UNIT
GROUPS = ((0, 512), (512, 512), (1024, 128))
UNIT_GROUPS = ((0, 4), (4, 4), (8, 1))
RAW_BUFS = 4
LOAD_PARTS = 1
TURNED = ((0, 0), (0, 1), (0, 2), (1, 0))
HALF = 2
SAMPLE_CUTS = ((0, 14), (14, 28), (28, 32), (14, 21), (21, 28))
RESULT_BYTES = NB * O_TILES * PIX * 4
RESULT_PLACES = (2, 3, 0, 2)
BY_PIXEL = (0, 1)

FLOPS = 2 * B * PIX * C_IN * C_OUT + 2 * B * C_OUT * C_OUT


def tile_joint_module_pa_t_kernel(
    tc, fv, ft, W1_words, W1_scales, b1, g1, be1, m1, v1, Wfc1, bfc1, out
):
    nc = tc.nc
    with ExitStack() as ctx:
        ctx.enter_context(tc.manual_schedule())
        const = ctx.enter_context(tc.tile_pool(name="const", bufs=1))
        big_pool = ctx.enter_context(tc.tile_pool(name="big", bufs=1))
        raw_pool = ctx.enter_context(tc.tile_pool(name="raw", bufs=RAW_BUFS))
        grouped_pool = ctx.enter_context(tc.tile_pool(name="grouped", bufs=3))
        mx_pool = ctx.enter_context(tc.tile_pool(name="mx", bufs=3))
        bank_pool = ctx.enter_context(tc.psum_pool(name="bank", bufs=8))

        def load_chunk_pass(chunk, g):
            raw = raw_pool.tile([P, NB, PACK * PIX], BF16, name="raw")
            for part in range(LOAD_PARTS):
                s0 = part * (NB // LOAD_PARTS)
                first = chunk * NB + s0
                nc.sync.dma_start(
                    out=raw[:, s0 : s0 + NB // LOAD_PARTS, :],
                    in_=fv[
                        first : first + NB // LOAD_PARTS, g * P * PACK : (g + 1) * P * PACK, :, :
                    ].rearrange("b (p t) h w -> p b (t h w)", t=PACK),
                )
            return raw

        prep_pool = tc.tile_pool(name="prep", bufs=1)
        with prep_pool as prep:
            whole = big_pool.tile([P, P * PACK * PIX], BF16, name="whole", offset=0)

            def load_turned(k):
                chunk, g = TURNED[k]
                nc.sync.dma_start(
                    out=whole[k : P : len(TURNED), :],
                    in_=fv[
                        chunk * NB : (chunk + 1) * NB, g * P * PACK : (g + 1) * P * PACK, :, :
                    ].rearrange("b c h w -> b (c h w)"),
                )

            vectors = (b1, g1, be1, m1, v1, bfc1)
            rows = prep.tile([P, C_OUT], BF16, name="rows")
            nc.gpsimd.memset(rows[:].bitcast(F32), 0.0)
            for v, vector in enumerate(vectors):
                if v % 3 == 0:
                    load_turned(v // 3)
                nc.sync.dma_start(out=rows[v : v + 1, :], in_=vector.rearrange("(r c) -> r c", r=1))
            ft_sb = prep.tile([P, C_OUT], BF16, name="ft_sb")
            nc.sync.dma_start(out=ft_sb[:], in_=ft)
            wfc_sb = prep.tile([P, O_TILES, C_OUT], BF16, name="wfc_sb")
            nc.sync.dma_start(out=wfc_sb[:], in_=Wfc1.rearrange("(p t) k -> p t k", t=O_TILES))
            w_raw = prep.tile([P, PASSES, 2 * C_OUT], U8, name="w_raw", align_bytes=64)
            nc.sync.dma_start(
                out=w_raw[:].bitcast(I32), in_=W1_words.bitcast(I32).rearrange("g p n -> p g n")
            )
            s_raw = prep.tile([P, PASSES, C_OUT], U8, name="s_raw", align_bytes=64)
            nc.vector.memset(s_raw[:].bitcast(I32), 0)
            for row in range(4):
                nc.sync.dma_start(
                    out=s_raw[row : P : 32].bitcast(I32),
                    in_=W1_scales[:, row:16:4, :].bitcast(I32).rearrange("g q n -> q g n"),
                )
            load_turned(2)
            load_turned(3)
            steps = [
                (chunk, g) for chunk in range(CHUNKS) for g in range(PASSES) if (chunk, g) not in TURNED
            ]
            raw_tiles = [load_chunk_pass(chunk, g) for chunk, g in steps[0:RAW_BUFS]]

            ident_bf = const.tile([P, P], BF16, name="ident_bf")
            make_identity(nc, ident_bf[:])
            ident_f32 = prep.tile([P, P], F32, name="ident_f32")
            make_identity(nc, ident_f32[:])
            to_slots = const.tile([P, P], F32, name="to_slots")
            nc.vector.tensor_copy(
                out=to_slots[:].rearrange("p (k b) -> p k b", b=NB),
                in_=ident_f32[:].rearrange("p (b k) -> p k b", b=NB),
            )
            bn_scale = const.tile([P, O_TILES], F32, name="bn_scale")
            bn_bias = const.tile([P, O_TILES], F32, name="bn_bias")
            gate = const.tile([P, O_TILES, B], F32, name="gate")
            rows_t = bank_pool.tile([P, O_TILES, P], BF16, name="rows_t", tag="bank")
            for ot in range(O_TILES):
                nc.tensor.transpose(rows_t[:, ot, :], rows[:, ot:C_OUT:O_TILES], ident_bf[:])
            per_channel = prep.tile([P, len(vectors), O_TILES], F32, name="per_channel")
            nc.vector.tensor_copy(
                out=per_channel[:].rearrange("p v t -> p t v"), in_=rows_t[:, :, 0 : len(vectors)]
            )
            b1_c, g1_c, be1_c, m1_c, v1_c, bfc1_c = [
                per_channel[:, v, :] for v in range(len(vectors))
            ]
            nc.vector.tensor_scalar_add(out=bn_scale[:], in0=v1_c, scalar1=EPS)
            nc.scalar.sqrt(out=bn_scale[:], in_=bn_scale[:])
            nc.vector.reciprocal(out=bn_scale[:], in_=bn_scale[:])
            nc.vector.tensor_mul(out=bn_scale[:], in0=bn_scale[:], in1=g1_c)
            nc.vector.tensor_sub(out=bn_bias[:], in0=b1_c, in1=m1_c)
            nc.vector.tensor_mul(out=bn_bias[:], in0=bn_bias[:], in1=bn_scale[:])
            nc.vector.tensor_add(out=bn_bias[:], in0=bn_bias[:], in1=be1_c)
            gate_bias = prep.tile([P, O_TILES], F32, name="gate_bias")
            nc.vector.tensor_scalar_add(out=gate_bias[:], in0=bfc1_c, scalar1=1.0)

            ft_t_ps = bank_pool.tile([P, K_TILES, P], BF16, name="ft_t_ps", tag="bank")
            for kt in range(K_TILES):
                nc.tensor.transpose(
                    ft_t_ps[:, kt, :], ft_sb[:, kt * P : (kt + 1) * P], ident_bf[:]
                )
            ft_t = prep.tile([P, K_TILES, P], BF16, name="ft_t")
            nc.vector.tensor_copy(out=ft_t[:], in_=ft_t_ps[:])
            wfc_t = prep.tile([P, K_TILES, C_OUT], BF16, name="wfc_t")
            for kt in range(K_TILES):
                wfc_t_ps = bank_pool.tile([P, O_TILES, P], BF16, name="wfc_t_ps", tag="bank")
                for ot in range(O_TILES):
                    nc.tensor.transpose(
                        wfc_t_ps[:, ot, :], wfc_sb[:, ot, kt * P : (kt + 1) * P], ident_bf[:]
                    )
                nc.vector.tensor_copy(
                    out=wfc_t[:, kt, :], in_=wfc_t_ps[:].rearrange("p t o -> p (t o)")
                )
            for ot in range(O_TILES):
                gate_ps = bank_pool.tile([P, B], F32, name="gate_ps", tag="bank")
                for kt in range(K_TILES):
                    nc.tensor.matmul(
                        gate_ps[:],
                        lhsT=wfc_t[:, kt, ot * P : (ot + 1) * P],
                        rhs=ft_t[:, kt, :],
                        start=(kt == 0),
                        stop=(kt == K_TILES - 1),
                    )
                nc.vector.tensor_scalar_add(
                    out=gate[:, ot, :], in0=gate_ps[:], scalar1=gate_bias[:, ot : ot + 1]
                )
            w_words = const.tile([P, PASSES, O_TILES, 2 * P], U8, name="w_words", align_bytes=64)
            w_scales = const.tile([P, PASSES, O_TILES, P], U8, name="w_scales", align_bytes=64)
            for g in range(PASSES):
                nc.vector.tensor_copy(
                    out=w_words[:, g].rearrange("p t (c b) -> p t c b", b=2),
                    in_=w_raw[:, g].rearrange("p (c t b) -> p t c b", t=O_TILES, b=2),
                )
                nc.gpsimd.tensor_copy(
                    out=w_scales[:, g],
                    in_=s_raw[:, g].rearrange("p (c t) -> p t c", t=O_TILES),
                )

        fv1_pool = ctx.enter_context(tc.tile_pool(name="fv1", bufs=2))

        by_word = whole[:].bitcast(F32).rearrange("b (p t j) -> b t j p", t=PACK, j=PIX // HALF)
        grouped_pairs = {}
        mx_tiles = {}
        fv1_tiles = {}
        result_tiles = {}

        def mx_tile(chunk):
            if chunk not in mx_tiles:
                mx_tiles[chunk] = (
                    mx_pool.tile([P, PASSES, CHUNK_COLS], U32, name="codes", align_bytes=64),
                    mx_pool.tile([P, PASSES, CHUNK_COLS], U8, name="scales", align_bytes=64),
                )
            return mx_tiles[chunk]

        def turn_pair(pair):
            grouped = grouped_pool.tile(
                [P, len(TURNED), 2, NB, QUAD, PACK], BF16, name="grouped", align_bytes=64
            )
            grouped_pairs[pair] = grouped
            for u, q in enumerate(range(2 * pair, min(2 * pair + 2, QUADS))):
                for half in range(QUAD // HALF):
                    bank = bank_pool.tile([P, PACK, P], F32, name="turned", tag="bank")
                    for t in range(PACK):
                        nc.tensor.transpose(
                            bank[:, t, :], by_word[:, t, q * (QUAD // HALF) + half, :], to_slots[:]
                        )
                    dst = grouped[:, :, u, :, half * HALF : (half + 1) * HALF, :]
                    src = (
                        bank[:]
                        .rearrange("p t c -> p (t c)")
                        .bitcast(BF16)
                        .rearrange("p (t k s l) -> p k s l t", t=PACK, k=len(TURNED), l=HALF)
                    )
                    if half == 1 and (pair < 2 or (pair == 2 and u == 0)):
                        nc.vector.tensor_copy(out=dst, in_=src)
                    else:
                        nc.scalar.copy(out=dst, in_=src)

        def quantise_pair(pair):
            grouped = grouped_pairs[pair]
            units = min(2, QUADS - 2 * pair)
            cols = slice(2 * pair * UNIT, (2 * pair + units) * UNIT)
            for k, (chunk, g) in enumerate(TURNED):
                codes, scales = mx_tile(chunk)
                nc.vector.quantize_mx(
                    out=codes[:, g, cols].bitcast(FP8X4),
                    scales=scales[:, g, cols],
                    in_=grouped[:, k, 0:units].rearrange("p u s l t -> p (u s l t)"),
                )

        flat_tiles = {}

        def regroup(step, vector_cuts, scalar_cuts):
            chunk, g = steps[step]
            raw = raw_tiles[step]
            if chunk in BY_PIXEL:
                grouped = grouped_pool.tile(
                    [P, QUADS, NB, QUAD, PACK], BF16, name="grouped", align_bytes=64
                )
                src = raw[:].rearrange("p s (t q l) -> p q s t l", t=PACK, l=QUAD)
                dst = grouped[:].rearrange("p q s l t -> p q s t l")
                flat = grouped[:].rearrange("p q s l t -> p (q s l t)")
            else:
                grouped = grouped_pool.tile(
                    [P, NB, QUADS, QUAD, PACK], BF16, name="grouped", align_bytes=64
                )
                src = raw[:].rearrange("p s (t q l) -> p s q t l", t=PACK, l=QUAD)
                dst = grouped[:].rearrange("p s q l t -> p s q t l")
                flat = grouped[:].rearrange("p s q l t -> p (s q l t)")
            for a, b in zip(vector_cuts, vector_cuts[1:]):
                nc.vector.tensor_copy(out=dst[:, a:b], in_=src[:, a:b])
            for a, b in zip(scalar_cuts, scalar_cuts[1:]):
                nc.scalar.copy(out=dst[:, a:b], in_=src[:, a:b])
            if step + RAW_BUFS < len(steps):
                raw_tiles.append(load_chunk_pass(*steps[step + RAW_BUFS]))
            flat_tiles[step] = flat

        def quantise(step):
            chunk, g = steps[step]
            codes, scales = mx_tile(chunk)
            for c0, n in GROUPS:
                nc.vector.quantize_mx(
                    out=codes[:, g, c0 : c0 + n].bitcast(FP8X4),
                    scales=scales[:, g, c0 : c0 + n],
                    in_=flat_tiles[step][:, PACK * c0 : PACK * (c0 + n)],
                )

        def convolve(chunk, group):
            codes, scales = mx_tiles[chunk]
            c0, n = GROUPS[group]
            q0, nq = UNIT_GROUPS[group]
            cols = slice(c0, c0 + n)
            if chunk in BY_PIXEL:
                fv1 = fv1_pool.tile([P, O_TILES, NB, nq * QUAD], F32, name="fv1p%d" % group, bufs=1)
                fv1_tiles[(chunk, group)] = fv1
            elif group == 0:
                if chunk == CHUNKS - 1:
                    fv1 = big_pool.tile(
                        [P, O_TILES, CHUNK_COLS], F32, name="fv1_last", offset=RESULT_BYTES
                    )
                else:
                    fv1 = fv1_pool.tile([P, O_TILES, CHUNK_COLS], F32, name="fv1", bufs=1)
                fv1_tiles[chunk] = fv1
            else:
                fv1 = fv1_tiles[chunk]
            accs = [bank_pool.tile([P, 512], F32, name="acc", tag="bank") for ot in range(O_TILES)]
            for g in range(PASSES):
                for ot in range(O_TILES):
                    nc.tensor.matmul_mx(
                        out=accs[ot][:, 0:n],
                        lhsT=w_words[:, g, ot].bitcast(FP4X4),
                        lhsT_scale=w_scales[:, g, ot],
                        rhs=codes[:, g, cols].bitcast(FP8X4),
                        rhs_scale=scales[:, g, cols],
                        start=(g == 0),
                        stop=(g == PASSES - 1),
                    )
            for ot in range(O_TILES):
                if chunk in BY_PIXEL:
                    dst = fv1[:, ot].rearrange("p s (q l) -> p q s l", l=QUAD)
                    src = accs[ot][:, 0:n].rearrange("p (q s l) -> p q s l", s=NB, l=QUAD)
                else:
                    dst = fv1[:, ot, cols]
                    src = accs[ot][:, 0:n]
                nc.scalar.activation(
                    out=dst,
                    in_=src,
                    func=ACT.Relu,
                    scale=bn_scale[:, ot : ot + 1],
                    bias=bn_bias[:, ot : ot + 1],
                )

        def multiply(chunk, group):
            if group == 0:
                result_tiles[chunk] = big_pool.tile(
                    [P, NB, O_TILES, PIX], F32, name="result%d" % chunk,
                    offset=RESULT_PLACES[chunk] * RESULT_BYTES,
                )
            result = result_tiles[chunk]
            if chunk in BY_PIXEL:
                q0, nq = UNIT_GROUPS[group]
                samples = slice(0, NB)
                pixels = slice(q0 * QUAD, (q0 + nq) * QUAD)
                in0 = fv1_tiles[(chunk, group)][:].rearrange("p t s x -> p s t x")
            else:
                samples = slice(*SAMPLE_CUTS[group])
                pixels = slice(0, PIX)
                in0 = fv1_tiles[chunk][:].rearrange("p t (s x) -> p s t x", x=PIX)[:, samples]
            ns = samples.stop - samples.start
            gate_bc = (
                gate[:, :, chunk * NB + samples.start : chunk * NB + samples.stop]
                .rearrange("p t s -> p s t")
                .unsqueeze(3)
                .to_broadcast([P, ns, O_TILES, pixels.stop - pixels.start])
            )
            nc.vector.tensor_tensor(
                out=result[:, samples, :, pixels], in0=in0, in1=gate_bc, op=ALU.mult
            )

        def store(chunk, s0, s1):
            first = chunk * NB
            nc.sync.dma_start(
                out=out[first + s0 : first + s1].rearrange(
                    "b (p t) h w -> p b (t h w)", t=O_TILES
                ),
                in_=result_tiles[chunk][:, s0:s1].rearrange("p s t x -> p s (t x)"),
            )

        def store_chunk(chunk, group):
            if chunk in BY_PIXEL:
                if group == PASSES - 1:
                    store(chunk, 0, NB)
            else:
                a, b = SAMPLE_CUTS[group]
                store(chunk, a, b)

        finished = []

        def finish(chunk, group):
            multiply(chunk, group)
            finished.append((chunk, group))
            if len(raw_tiles) == len(steps):
                for pair in finished:
                    store_chunk(*pair)
                finished.clear()

        pix = lambda n: ((0, 4, n) if n > 4 else (0, 4), tuple(range(n, QUADS + 1)))
        smp = lambda n: ((0, n), (n, 29, 32))
        turn_pair(0)
        turn_pair(1)
        quantise_pair(0)
        turn_pair(2)
        quantise_pair(1)
        regroup(0, *pix(8))
        quantise(0)
        turn_pair(3)
        quantise_pair(2)
        convolve(0, 0)
        turn_pair(4)
        quantise_pair(3)
        regroup(1, *pix(8))
        quantise(1)
        convolve(0, 1)
        finish(0, 0)
        quantise_pair(4)
        convolve(0, 2)
        regroup(2, *smp(18))
        finish(0, 1)
        quantise(2)
        convolve(1, 0)
        regroup(3, *smp(16))
        finish(0, 2)
        quantise(3)
        for i in range(4, 8):
            convolve(*divmod(i, 3))
            regroup(i, *smp(16))
            finish(*divmod(i - 1, 3))
            quantise(i)
        convolve(2, 2)
        finish(2, 1)
        convolve(3, 0)
        finish(2, 2)
        convolve(3, 1)
        finish(3, 0)
        convolve(3, 2)
        finish(3, 3)
        finish(3, 4)
        finish(3, 2)
